import numpy as np
import ml_dtypes


def mxq(x, axis, fmt="e4m3"):
    dtype, down = {"e4m3": (ml_dtypes.float8_e4m3fn, 7), "e5m2": (ml_dtypes.float8_e5m2, 14)}[fmt]
    v = np.moveaxis(np.asarray(x, np.float32).astype(ml_dtypes.bfloat16).astype(np.float64), axis, -1)
    blocks = v.reshape(v.shape[:-1] + (-1, 32))
    amax = np.abs(blocks).max(-1, keepdims=True)
    byte = np.maximum(np.where(amax > 0, np.frexp(amax)[1] - 1 + 127, 0) - down, 1)
    scale = np.exp2(byte - 127.0)
    codes = (blocks / scale).astype(np.float32).astype(dtype).astype(np.float64)
    return np.moveaxis((codes * scale).reshape(v.shape), -1, axis)


WIDE = False


def mx_kscale(k):
    if not WIDE:
        return np.ones(k)
    levels = np.array([10, -10, 5, -5, 0])
    a = np.random.permutation(np.resize(levels, k // 512 * 4)).reshape(k // 512, 4)
    idx = np.arange(k)
    return np.exp2(a[idx // 512, idx % 128 // 32])


BF16 = ml_dtypes.bfloat16


def bf(x):
    return np.asarray(x, np.float32).astype(BF16)


def f64(x):
    return np.asarray(x).astype(np.float64)


B, D_IN, D_HID, SHARE = 1024, 512, 256, 2
NUM_GATE = 4 + SHARE


def sigmoid(v):
    return 1.0 / (1.0 + np.exp(-v))


def setup_inputs():
    s = mx_kscale(D_IN)
    n = np.random.standard_normal
    return {
        "input": bf(n((B, D_IN)) * s),
        "h_minors": bf(n((B, D_HID))),
        "c_minors": bf(n((B, D_HID))),
        "s_minors": bf(n((SHARE, B, D_HID))),
        "mask": bf(np.random.uniform(0.5, 1.5, B)),
        "weight_ih": bf(n((NUM_GATE * D_HID, D_IN)) * 0.7 / np.sqrt(D_IN) / s),
        "weight_hh": bf(n((4 * D_HID, D_HID)) * 0.7 / np.sqrt(D_HID)),
        "weight_sh": bf(n((SHARE * D_HID, D_HID)) * 0.7 / np.sqrt(D_HID)),
        "bias_ih": bf(n(NUM_GATE * D_HID) * 0.3),
        "bias_hh": bf(n(4 * D_HID) * 0.3),
        "bias_sh": bf(n(SHARE * D_HID) * 0.3),
        "idx": 0,
    }


def reference(input, h_minors, c_minors, s_minors, mask, weight_ih, weight_hh, weight_sh, bias_ih, bias_hh, bias_sh, idx):
    H = weight_hh.shape[1]
    share = weight_sh.shape[0] // H
    m = f64(mask)[:, None]
    tmp = (mxq(f64(input), 1, "e4m3") @ mxq(f64(weight_ih), 1, "e4m3").T) + f64(bias_ih)
    tmp2 = f64(h_minors) @ f64(weight_hh).T + f64(bias_hh)
    tmp3 = f64(s_minors)[idx] @ f64(weight_sh).T + f64(bias_sh)
    tmp_in, tmp_s = tmp[:, :4 * H], tmp[:, 4 * H:]
    z = tmp_in + tmp2
    ifo = sigmoid(z[:, :3 * H])
    i, f, o = ifo[:, :H], ifo[:, H:2 * H], ifo[:, 2 * H:]
    c_hat = z[:, 3 * H:]
    b = sigmoid(tmp_s + tmp3)
    c_t = (f * f64(c_minors) + i * np.tanh(c_hat)) * m
    tc = np.tanh(c_t) * m
    h = o * tc
    s = b.reshape(-1, share, H) * tc[:, None, :]
    s = np.moveaxis(s, 1, 0)
    return (h, c_t, s[0], s[1])

@@ -1,0 +1,303 @@
+from contextlib import ExitStack
+
+import concourse.mybir as mybir
+from concourse.masks import make_identity
+
+FP8X4 = mybir.dt.float8_e4m3fn_x4
+BF16 = mybir.dt.bfloat16
+F32 = mybir.dt.float32
+U32 = mybir.dt.uint32
+U8 = mybir.dt.uint8
+ACT = mybir.ActivationFunctionType
+ALU = mybir.AluOpType
+
+P = 128
+PACK = 4
+BATCH = 1024
+D_IN = 512
+HID = 256
+N_TILES = BATCH // P
+WORDS = D_IN // 2
+K_CHUNKS = HID // P
+PAIR_COLS = 2 * HID
+STORE_TILES = 2
+
+GATE_PAIRS = ((0, 3), (1, 2), (4, 5))
+N_GATES = 6
+N_RECURRENT = 4
+
+FLOPS = 2 * BATCH * (D_IN * N_GATES * HID + HID * N_GATES * HID)
+BYTES = (
+    2 * (BATCH * D_IN + 3 * BATCH * HID + BATCH)
+    + 2 * (N_GATES * HID * (D_IN + HID) + 2 * N_GATES * HID)
+    + 4 * 4 * BATCH * HID
+)
+
+
+def tile_share_lstm_cell_kernel(
+    tc,
+    x,
+    h_minors,
+    c_minors,
+    s_minors,
+    mask,
+    weight_ih,
+    weight_hh,
+    weight_sh,
+    bias_ih,
+    bias_hh,
+    bias_sh,
+    idx,
+    out_h,
+    out_c,
+    out_s0,
+    out_s1,
+):
+    nc = tc.nc
+
+    def by_batch_tile(dram):
+        return dram.rearrange("(p t) n -> p t n", t=N_TILES)
+
+    def by_row_block(dram):
+        return dram.rearrange("(r p) n -> p r n", p=P)
+
+    with ExitStack() as ctx:
+        keep = ctx.enter_context(tc.tile_pool(name="keep", bufs=1))
+        stage = ctx.enter_context(tc.tile_pool(name="stage", bufs=3))
+        turn_psum = ctx.enter_context(tc.psum_pool(name="turn_psum", bufs=2))
+        mx_psum = ctx.enter_context(tc.psum_pool(name="mx_psum", bufs=3))
+        plain_psum = ctx.enter_context(tc.psum_pool(name="plain_psum", bufs=3))
+
+        ident_f32 = keep.tile([P, P], F32)
+        make_identity(nc, ident_f32[:])
+        ident_bf16 = keep.tile([P, P], BF16)
+        make_identity(nc, ident_bf16[:])
+        ones = keep.tile([P, P], BF16)
+        nc.vector.memset(ones[:], 1.0)
+        warm = keep.tile([P, 1], F32)
+        nc.vector.memset(warm[:], 0.0)
+        nc.scalar.activation(out=warm[:], in_=warm[:], func=ACT.Sigmoid)
+
+        x_sb = keep.tile([P, N_TILES * D_IN], BF16)
+        h_sb = keep.tile([P, N_TILES * HID], BF16)
+        s_sb = keep.tile([P, N_TILES * HID], BF16)
+        c_sb = keep.tile([P, N_TILES * HID], BF16)
+        w_in_sb = keep.tile([P, N_GATES * 2 * D_IN], BF16)
+        w_rec_sb = keep.tile([P, N_GATES * 2 * HID], BF16)
+        mask_sb = keep.tile([P, N_TILES], BF16)
+        bias_rows = keep.tile([P, N_GATES * HID], BF16)
+        nc.vector.memset(bias_rows[:], 0.0)
+
+        def load_batch(tile_sb, dram, first, count):
+            view = tile_sb[:].rearrange("p (t n) -> p t n", t=N_TILES)
+            nc.sync.dma_start(
+                out=view[:, first : first + count, :],
+                in_=by_batch_tile(dram)[:, first : first + count, :],
+            )
+
+        def load_weights(pair):
+            for half in range(2):
+                gate = GATE_PAIRS[pair][half]
+                place = 2 * pair + half
+                nc.sync.dma_start(
+                    out=w_in_sb[:, place * 2 * D_IN : (place + 1) * 2 * D_IN].rearrange(
+                        "p (r n) -> p r n", r=2
+                    ),
+                    in_=by_row_block(weight_ih[gate * HID : (gate + 1) * HID, :]),
+                )
+            for half in range(2):
+                gate = GATE_PAIRS[pair][half]
+                place = 2 * pair + half
+                if gate < N_RECURRENT:
+                    rows = weight_hh[gate * HID : (gate + 1) * HID, :]
+                else:
+                    rows = weight_sh[(gate - N_RECURRENT) * HID : (gate - N_RECURRENT + 1) * HID, :]
+                nc.sync.dma_start(
+                    out=w_rec_sb[:, place * 2 * HID : (place + 1) * 2 * HID].rearrange(
+                        "p (r n) -> p r n", r=2
+                    ),
+                    in_=by_row_block(rows),
+                )
+
+        load_weights(0)
+        load_batch(x_sb, x, 0, N_TILES // 2)
+        load_batch(h_sb, h_minors, 0, N_TILES)
+        load_batch(x_sb, x, N_TILES // 2, N_TILES // 2)
+        nc.sync.dma_start(out=bias_rows[0:1, :], in_=bias_ih.rearrange("(o n) -> o n", o=1))
+        nc.sync.dma_start(
+            out=bias_rows[1:2, 0 : N_RECURRENT * HID], in_=bias_hh.rearrange("(o n) -> o n", o=1)
+        )
+        nc.sync.dma_start(
+            out=bias_rows[1:2, N_RECURRENT * HID :], in_=bias_sh.rearrange("(o n) -> o n", o=1)
+        )
+        load_weights(1)
+        load_batch(c_sb, c_minors, 0, N_TILES)
+        nc.sync.dma_start(out=mask_sb[:], in_=mask.rearrange("(p t) -> p t", t=N_TILES))
+        load_weights(2)
+        load_batch(s_sb, s_minors[idx, :, :], 0, N_TILES)
+
+        bias_all = keep.tile([P, N_GATES * HID], F32)
+        for pair in range(3):
+            spread = plain_psum.tile([P, PAIR_COLS], F32, tag="acc_plain")
+            for half in range(2):
+                gate = GATE_PAIRS[pair][half]
+                nc.tensor.matmul(
+                    out=spread[:, half * HID : (half + 1) * HID],
+                    lhsT=ones[:],
+                    rhs=bias_rows[:, gate * HID : (gate + 1) * HID],
+                    start=True,
+                    stop=True,
+                )
+            nc.scalar.copy(out=bias_all[:, pair * PAIR_COLS : (pair + 1) * PAIR_COLS], in_=spread[:])
+
+        mask_f32 = keep.tile([P, N_TILES], F32)
+        nc.vector.tensor_copy(out=mask_f32[:], in_=mask_sb[:])
+
+        x_codes = keep.tile([P, N_TILES * P], U32, align_bytes=64)
+        x_scales = keep.tile([P, N_TILES * P], U8, align_bytes=64)
+        w_codes = keep.tile([P, N_GATES * HID], U32, align_bytes=64)
+        w_scales = keep.tile([P, N_GATES * HID], U8, align_bytes=64)
+
+        def quantise_two_blocks(source_sb, codes, scales, first_block, copy_out):
+            words = source_sb[:].bitcast(F32)
+            turned = turn_psum.tile([P, 2, 2, P], F32, tag="turned")
+            for j in range(2):
+                for u in range(2):
+                    first = (first_block + j) * WORDS + u * P
+                    nc.tensor.transpose(turned[:, j, u, :], words[:, first : first + P], ident_f32[:])
+            grouped = stage.tile([P, 2 * P * PACK], BF16, align_bytes=64)
+            copy_out(
+                out=grouped[:].bitcast(F32).rearrange("p (j r u) -> p j r u", j=2, u=2),
+                in_=turned[:].rearrange("p j u r -> p j r u"),
+            )
+            cols = slice(first_block * P, (first_block + 2) * P)
+            nc.vector.quantize_mx(
+                out=codes[:, cols].bitcast(FP8X4), scales=scales[:, cols], in_=grouped[:]
+            )
+
+        def turn_four_squares(squares, dest, copy_out):
+            turned = turn_psum.tile([P, 2, 2 * P], BF16, tag="turned")
+            for i in range(4):
+                nc.tensor.transpose(
+                    turned[:, i // 2, (i % 2) * P : (i % 2 + 1) * P], squares[i], ident_bf16[:]
+                )
+            copy_out(out=dest, in_=turned[:])
+
+        h_T = keep.tile([P, N_TILES, HID], BF16)
+        s_T = keep.tile([P, N_TILES, HID], BF16)
+        w_rec_T = keep.tile([P, 3, K_CHUNKS, PAIR_COLS], BF16)
+
+        def turn_state(state_sb, state_T, first_tile, copy_out):
+            squares = [
+                state_sb[:, (first_tile + j) * HID + c * P : (first_tile + j) * HID + (c + 1) * P]
+                for j in range(2)
+                for c in range(K_CHUNKS)
+            ]
+            turn_four_squares(squares, state_T[:, first_tile : first_tile + 2, :], copy_out)
+
+        def prepare_weights(pair):
+            for half in range(2):
+                place = 2 * pair + half
+                quantise_two_blocks(w_in_sb, w_codes, w_scales, 2 * place, nc.scalar.copy)
+            for half in range(2):
+                place = 2 * pair + half
+                squares = [
+                    w_rec_sb[:, (2 * place + r) * HID + c * P : (2 * place + r) * HID + (c + 1) * P]
+                    for c in range(K_CHUNKS)
+                    for r in range(2)
+                ]
+                turn_four_squares(
+                    squares, w_rec_T[:, pair, :, half * HID : (half + 1) * HID], nc.scalar.copy
+                )
+
+        def pre_activation(pair, t):
+            state_T = h_T if GATE_PAIRS[pair][0] < N_RECURRENT else s_T
+            cols = slice(pair * PAIR_COLS, (pair + 1) * PAIR_COLS)
+            rows = slice(t * P, (t + 1) * P)
+            acc_plain = plain_psum.tile([P, PAIR_COLS], F32, tag="acc_plain")
+            for c in range(K_CHUNKS):
+                nc.tensor.matmul(
+                    out=acc_plain[:],
+                    lhsT=state_T[:, t, c * P : (c + 1) * P],
+                    rhs=w_rec_T[:, pair, c, :],
+                    start=(c == 0),
+                    stop=(c == K_CHUNKS - 1),
+                )
+            acc_mx = mx_psum.tile([P, PAIR_COLS], F32)
+            nc.tensor.matmul_mx(
+                out=acc_mx[:],
+                lhsT=x_codes[:, rows].bitcast(FP8X4),
+                lhsT_scale=x_scales[:, rows],
+                rhs=w_codes[:, cols].bitcast(FP8X4),
+                rhs_scale=w_scales[:, cols],
+                start=True,
+                stop=True,
+            )
+            partial = stage.tile([P, PAIR_COLS], F32)
+            nc.vector.tensor_tensor(out=partial[:], in0=acc_plain[:], in1=bias_all[:, cols], op=ALU.add)
+            pre = stage.tile([P, PAIR_COLS], F32)
+            nc.vector.tensor_tensor(out=pre[:], in0=acc_mx[:], in1=partial[:], op=ALU.add)
+            return pre
+
+        def store(dram, result, t):
+            if t % STORE_TILES == STORE_TILES - 1:
+                group = slice(t + 1 - STORE_TILES, t + 1)
+                nc.sync.dma_start(out=by_batch_tile(dram)[:, group, :], in_=result[:, group, :])
+
+        in_term = keep.tile([P, N_TILES, HID], F32)
+        tanh_cell = keep.tile([P, N_TILES, HID], F32)
+        h_res = keep.tile([P, N_TILES, HID], F32)
+        c_res = keep.tile([P, N_TILES, HID], F32)
+        s_res = keep.tile([P, 2, N_TILES, HID], F32)
+        c_tiles = c_sb[:].rearrange("p (t n) -> p t n", t=N_TILES)
+
+        prepare_weights(0)
+        for first_tile in range(0, N_TILES, 2):
+            quantise_two_blocks(x_sb, x_codes, x_scales, first_tile, nc.vector.tensor_copy)
+            turn_state(h_sb, h_T, first_tile, nc.vector.tensor_copy)
+        prepare_weights(1)
+
+        for t in range(N_TILES):
+            pre = pre_activation(0, t)
+            gates = stage.tile([P, PAIR_COLS], F32)
+            nc.scalar.activation(out=gates[:, 0:HID], in_=pre[:, 0:HID], func=ACT.Sigmoid)
+            nc.scalar.activation(out=gates[:, HID:], in_=pre[:, HID:], func=ACT.Tanh)
+            nc.gpsimd.tensor_tensor(
+                out=in_term[:, t, :], in0=gates[:, 0:HID], in1=gates[:, HID:], op=ALU.mult
+            )
+
+        prepare_weights(2)
+        for first_tile in range(0, N_TILES, 2):
+            turn_state(s_sb, s_T, first_tile, nc.scalar.copy)
+
+        for t in range(N_TILES):
+            m = mask_f32[:, t : t + 1]
+            pre = pre_activation(1, t)
+            gates = stage.tile([P, PAIR_COLS], F32)
+            nc.scalar.activation(out=gates[:], in_=pre[:], func=ACT.Sigmoid)
+            kept = stage.tile([P, HID], F32)
+            nc.gpsimd.tensor_tensor(out=kept[:], in0=gates[:, 0:HID], in1=c_tiles[:, t, :], op=ALU.mult)
+            cell = stage.tile([P, HID], F32)
+            nc.vector.tensor_tensor(out=cell[:], in0=kept[:], in1=in_term[:, t, :], op=ALU.add)
+            nc.scalar.activation(out=c_res[:, t, :], in_=cell[:], func=ACT.Copy, scale=m)
+            store(out_c, c_res, t)
+            squashed = stage.tile([P, HID], F32)
+            nc.scalar.activation(out=squashed[:], in_=cell[:], func=ACT.Tanh, scale=m)
+            nc.scalar.activation(out=tanh_cell[:, t, :], in_=squashed[:], func=ACT.Copy, scale=m)
+            nc.gpsimd.tensor_tensor(
+                out=h_res[:, t, :], in0=gates[:, HID:], in1=tanh_cell[:, t, :], op=ALU.mult
+            )
+            store(out_h, h_res, t)
+
+        for t in range(N_TILES):
+            pre = pre_activation(2, t)
+            gates = stage.tile([P, PAIR_COLS], F32)
+            nc.scalar.activation(out=gates[:], in_=pre[:], func=ACT.Sigmoid)
+            nc.gpsimd.tensor_tensor(
+                out=s_res[:, :, t, :],
+                in0=gates[:].rearrange("p (g n) -> p g n", g=2),
+                in1=tanh_cell[:, t, :].unsqueeze(1).to_broadcast([P, 2, HID]),
+                op=ALU.mult,
+            )
+            store(out_s0, s_res[:, 0, :, :], t)
+            store(out_s1, s_res[:, 1, :, :], t)

@@ -19,12 +19,12 @@ HID = 256
 N_TILES = BATCH // P
 WORDS = D_IN // 2
 K_CHUNKS = HID // P
-PAIR_COLS = 2 * HID
-STORE_TILES = 2
-
-GATE_PAIRS = ((0, 3), (1, 2), (4, 5))
 N_GATES = 6
+N_PAIRS = N_GATES // 2
 N_RECURRENT = 4
+PAIR_COLS = 2 * HID
+PSUM_BANKS = 8
+STORE_TILES = 2
 
 FLOPS = 2 * BATCH * (D_IN * N_GATES * HID + HID * N_GATES * HID)
 BYTES = (
@@ -58,20 +58,18 @@ def tile_share_lstm_cell_kernel(
     def by_batch_tile(dram):
         return dram.rearrange("(p t) n -> p t n", t=N_TILES)
 
-    def by_row_block(dram):
-        return dram.rearrange("(r p) n -> p r n", p=P)
+    def as_row(vector):
+        return vector.rearrange("(o n) -> o n", o=1)
 
     with ExitStack() as ctx:
         keep = ctx.enter_context(tc.tile_pool(name="keep", bufs=1))
-        stage = ctx.enter_context(tc.tile_pool(name="stage", bufs=3))
-        turn_psum = ctx.enter_context(tc.psum_pool(name="turn_psum", bufs=2))
-        mx_psum = ctx.enter_context(tc.psum_pool(name="mx_psum", bufs=3))
-        plain_psum = ctx.enter_context(tc.psum_pool(name="plain_psum", bufs=3))
+        stage = ctx.enter_context(tc.tile_pool(name="stage", bufs=4))
+        psum = ctx.enter_context(tc.psum_pool(name="psum", bufs=PSUM_BANKS))
 
         ident_f32 = keep.tile([P, P], F32)
         make_identity(nc, ident_f32[:])
         ident_bf16 = keep.tile([P, P], BF16)
-        make_identity(nc, ident_bf16[:])
+        nc.vector.tensor_copy(out=ident_bf16[:], in_=ident_f32[:])
         ones = keep.tile([P, P], BF16)
         nc.vector.memset(ones[:], 1.0)
         warm = keep.tile([P, 1], F32)
@@ -81,7 +79,7 @@ def tile_share_lstm_cell_kernel(
         x_sb = keep.tile([P, N_TILES * D_IN], BF16)
         h_sb = keep.tile([P, N_TILES * HID], BF16)
         s_sb = keep.tile([P, N_TILES * HID], BF16)
-        c_sb = keep.tile([P, N_TILES * HID], BF16)
+        c_sb = keep.tile([P, N_TILES, HID], BF16)
         w_in_sb = keep.tile([P, N_GATES * 2 * D_IN], BF16)
         w_rec_sb = keep.tile([P, N_GATES * 2 * HID], BF16)
         mask_sb = keep.tile([P, N_TILES], BF16)
@@ -95,72 +93,56 @@ def tile_share_lstm_cell_kernel(
                 in_=by_batch_tile(dram)[:, first : first + count, :],
             )
 
-        def load_weights(pair):
-            for half in range(2):
-                gate = GATE_PAIRS[pair][half]
-                place = 2 * pair + half
-                nc.sync.dma_start(
-                    out=w_in_sb[:, place * 2 * D_IN : (place + 1) * 2 * D_IN].rearrange(
-                        "p (r n) -> p r n", r=2
-                    ),
-                    in_=by_row_block(weight_ih[gate * HID : (gate + 1) * HID, :]),
-                )
-            for half in range(2):
-                gate = GATE_PAIRS[pair][half]
-                place = 2 * pair + half
-                if gate < N_RECURRENT:
-                    rows = weight_hh[gate * HID : (gate + 1) * HID, :]
-                else:
-                    rows = weight_sh[(gate - N_RECURRENT) * HID : (gate - N_RECURRENT + 1) * HID, :]
-                nc.sync.dma_start(
-                    out=w_rec_sb[:, place * 2 * HID : (place + 1) * 2 * HID].rearrange(
-                        "p (r n) -> p r n", r=2
-                    ),
-                    in_=by_row_block(rows),
-                )
+        def load_gate(tile_sb, rows, gate):
+            width = rows.shape[1]
+            nc.sync.dma_start(
+                out=tile_sb[:, gate * 2 * width : (gate + 1) * 2 * width].rearrange(
+                    "p (r n) -> p r n", r=2
+                ),
+                in_=rows.rearrange("(r p) n -> p r n", p=P),
+            )
 
+        def load_weights(pair):
+            for gate in (2 * pair, 2 * pair + 1):
+                load_gate(w_in_sb, weight_ih[gate * HID : (gate + 1) * HID, :], gate)
+            for gate in (2 * pair, 2 * pair + 1):
+                if gate < N_RECURRENT:
+                    load_gate(w_rec_sb, weight_hh[gate * HID : (gate + 1) * HID, :], gate)
+                else:
+                    share = gate - N_RECURRENT
+                    load_gate(w_rec_sb, weight_sh[share * HID : (share + 1) * HID, :], gate)
+
+        nc.scalar.dma_start(out=bias_rows[0:1, :], in_=as_row(bias_ih))
+        nc.scalar.dma_start(out=bias_rows[1:2, 0 : N_RECURRENT * HID], in_=as_row(bias_hh))
+        nc.scalar.dma_start(out=bias_rows[1:2, N_RECURRENT * HID :], in_=as_row(bias_sh))
         load_weights(0)
-        load_batch(x_sb, x, 0, N_TILES // 2)
-        load_batch(h_sb, h_minors, 0, N_TILES)
-        load_batch(x_sb, x, N_TILES // 2, N_TILES // 2)
-        nc.sync.dma_start(out=bias_rows[0:1, :], in_=bias_ih.rearrange("(o n) -> o n", o=1))
-        nc.sync.dma_start(
-            out=bias_rows[1:2, 0 : N_RECURRENT * HID], in_=bias_hh.rearrange("(o n) -> o n", o=1)
-        )
-        nc.sync.dma_start(
-            out=bias_rows[1:2, N_RECURRENT * HID :], in_=bias_sh.rearrange("(o n) -> o n", o=1)
-        )
+        for first_tile in range(0, N_TILES, 2):
+            load_batch(x_sb, x, first_tile, 2)
+            load_batch(h_sb, h_minors, first_tile, 2)
         load_weights(1)
-        load_batch(c_sb, c_minors, 0, N_TILES)
         nc.sync.dma_start(out=mask_sb[:], in_=mask.rearrange("(p t) -> p t", t=N_TILES))
+        nc.sync.dma_start(out=c_sb[:], in_=by_batch_tile(c_minors))
         load_weights(2)
         load_batch(s_sb, s_minors[idx, :, :], 0, N_TILES)
 
         bias_all = keep.tile([P, N_GATES * HID], F32)
-        for pair in range(3):
-            spread = plain_psum.tile([P, PAIR_COLS], F32, tag="acc_plain")
-            for half in range(2):
-                gate = GATE_PAIRS[pair][half]
-                nc.tensor.matmul(
-                    out=spread[:, half * HID : (half + 1) * HID],
-                    lhsT=ones[:],
-                    rhs=bias_rows[:, gate * HID : (gate + 1) * HID],
-                    start=True,
-                    stop=True,
-                )
-            nc.scalar.copy(out=bias_all[:, pair * PAIR_COLS : (pair + 1) * PAIR_COLS], in_=spread[:])
-
-        mask_f32 = keep.tile([P, N_TILES], F32)
-        nc.vector.tensor_copy(out=mask_f32[:], in_=mask_sb[:])
+        for pair in range(N_PAIRS):
+            cols = slice(pair * PAIR_COLS, (pair + 1) * PAIR_COLS)
+            spread = psum.tile([P, PAIR_COLS], F32, tag="bank")
+            nc.tensor.matmul(out=spread[:], lhsT=ones[:], rhs=bias_rows[:, cols], start=True, stop=True)
+            nc.vector.tensor_copy(out=bias_all[:, cols], in_=spread[:])
 
         x_codes = keep.tile([P, N_TILES * P], U32, align_bytes=64)
         x_scales = keep.tile([P, N_TILES * P], U8, align_bytes=64)
         w_codes = keep.tile([P, N_GATES * HID], U32, align_bytes=64)
         w_scales = keep.tile([P, N_GATES * HID], U8, align_bytes=64)
+        h_T = keep.tile([P, N_TILES, HID], BF16)
+        s_T = keep.tile([P, N_TILES, HID], BF16)
+        w_rec_T = keep.tile([P, N_PAIRS, K_CHUNKS, PAIR_COLS], BF16)
 
         def quantise_two_blocks(source_sb, codes, scales, first_block, copy_out):
             words = source_sb[:].bitcast(F32)
-            turned = turn_psum.tile([P, 2, 2, P], F32, tag="turned")
+            turned = psum.tile([P, 2, 2, P], F32, tag="bank")
             for j in range(2):
                 for u in range(2):
                     first = (first_block + j) * WORDS + u * P
@@ -176,16 +158,12 @@ def tile_share_lstm_cell_kernel(
             )
 
         def turn_four_squares(squares, dest, copy_out):
-            turned = turn_psum.tile([P, 2, 2 * P], BF16, tag="turned")
+            turned = psum.tile([P, 2, 2 * P], BF16, tag="bank")
             for i in range(4):
                 nc.tensor.transpose(
                     turned[:, i // 2, (i % 2) * P : (i % 2 + 1) * P], squares[i], ident_bf16[:]
                 )
             copy_out(out=dest, in_=turned[:])
-
-        h_T = keep.tile([P, N_TILES, HID], BF16)
-        s_T = keep.tile([P, N_TILES, HID], BF16)
-        w_rec_T = keep.tile([P, 3, K_CHUNKS, PAIR_COLS], BF16)
 
         def turn_state(state_sb, state_T, first_tile, copy_out):
             squares = [
@@ -195,26 +173,29 @@ def tile_share_lstm_cell_kernel(
             ]
             turn_four_squares(squares, state_T[:, first_tile : first_tile + 2, :], copy_out)
 
-        def prepare_weights(pair):
-            for half in range(2):
-                place = 2 * pair + half
-                quantise_two_blocks(w_in_sb, w_codes, w_scales, 2 * place, nc.scalar.copy)
-            for half in range(2):
-                place = 2 * pair + half
-                squares = [
-                    w_rec_sb[:, (2 * place + r) * HID + c * P : (2 * place + r) * HID + (c + 1) * P]
-                    for c in range(K_CHUNKS)
-                    for r in range(2)
-                ]
-                turn_four_squares(
-                    squares, w_rec_T[:, pair, :, half * HID : (half + 1) * HID], nc.scalar.copy
-                )
+        def prepare_inputs(first_tile, copy_x, copy_h):
+            quantise_two_blocks(x_sb, x_codes, x_scales, first_tile, copy_x)
+            turn_state(h_sb, h_T, first_tile, copy_h)
 
-        def pre_activation(pair, t):
-            state_T = h_T if GATE_PAIRS[pair][0] < N_RECURRENT else s_T
+        def prepare_gate(gate, copy_in, copy_rec):
+            quantise_two_blocks(w_in_sb, w_codes, w_scales, 2 * gate, copy_in)
+            squares = [
+                w_rec_sb[:, (2 * gate + r) * HID + c * P : (2 * gate + r) * HID + (c + 1) * P]
+                for c in range(K_CHUNKS)
+                for r in range(2)
+            ]
+            half = gate % 2
+            turn_four_squares(
+                squares, w_rec_T[:, gate // 2, :, half * HID : (half + 1) * HID], copy_rec
+            )
+
+        gates = keep.tile([P, N_PAIRS, N_TILES, PAIR_COLS], F32)
+
+        def gate_values(pair, t):
+            state_T = h_T if 2 * pair < N_RECURRENT else s_T
             cols = slice(pair * PAIR_COLS, (pair + 1) * PAIR_COLS)
             rows = slice(t * P, (t + 1) * P)
-            acc_plain = plain_psum.tile([P, PAIR_COLS], F32, tag="acc_plain")
+            acc_plain = psum.tile([P, PAIR_COLS], F32, tag="bank")
             for c in range(K_CHUNKS):
                 nc.tensor.matmul(
                     out=acc_plain[:],
@@ -223,7 +204,7 @@ def tile_share_lstm_cell_kernel(
                     start=(c == 0),
                     stop=(c == K_CHUNKS - 1),
                 )
-            acc_mx = mx_psum.tile([P, PAIR_COLS], F32)
+            acc_mx = psum.tile([P, PAIR_COLS], F32, tag="bank")
             nc.tensor.matmul_mx(
                 out=acc_mx[:],
                 lhsT=x_codes[:, rows].bitcast(FP8X4),
@@ -237,67 +218,94 @@ def tile_share_lstm_cell_kernel(
             nc.vector.tensor_tensor(out=partial[:], in0=acc_plain[:], in1=bias_all[:, cols], op=ALU.add)
             pre = stage.tile([P, PAIR_COLS], F32)
             nc.vector.tensor_tensor(out=pre[:], in0=acc_mx[:], in1=partial[:], op=ALU.add)
-            return pre
+            if pair == 1:
+                nc.scalar.activation(out=gates[:, pair, t, 0:HID], in_=pre[:, 0:HID], func=ACT.Sigmoid)
+                nc.scalar.activation(out=gates[:, pair, t, HID:], in_=pre[:, HID:], func=ACT.Tanh)
+            else:
+                nc.scalar.activation(out=gates[:, pair, t, :], in_=pre[:], func=ACT.Sigmoid)
 
         def store(dram, result, t):
             if t % STORE_TILES == STORE_TILES - 1:
                 group = slice(t + 1 - STORE_TILES, t + 1)
                 nc.sync.dma_start(out=by_batch_tile(dram)[:, group, :], in_=result[:, group, :])
 
-        in_term = keep.tile([P, N_TILES, HID], F32)
+        mask_f32 = keep.tile([P, N_TILES], F32)
+        c_masked = keep.tile([P, N_TILES, HID], F32)
+        kept = keep.tile([P, N_TILES, HID], F32)
         tanh_cell = keep.tile([P, N_TILES, HID], F32)
         h_res = keep.tile([P, N_TILES, HID], F32)
         c_res = keep.tile([P, N_TILES, HID], F32)
         s_res = keep.tile([P, 2, N_TILES, HID], F32)
-        c_tiles = c_sb[:].rearrange("p (t n) -> p t n", t=N_TILES)
 
-        prepare_weights(0)
-        for first_tile in range(0, N_TILES, 2):
-            quantise_two_blocks(x_sb, x_codes, x_scales, first_tile, nc.vector.tensor_copy)
-            turn_state(h_sb, h_T, first_tile, nc.vector.tensor_copy)
-        prepare_weights(1)
-
-        for t in range(N_TILES):
-            pre = pre_activation(0, t)
-            gates = stage.tile([P, PAIR_COLS], F32)
-            nc.scalar.activation(out=gates[:, 0:HID], in_=pre[:, 0:HID], func=ACT.Sigmoid)
-            nc.scalar.activation(out=gates[:, HID:], in_=pre[:, HID:], func=ACT.Tanh)
+        def after_input_and_forget(t):
             nc.gpsimd.tensor_tensor(
-                out=in_term[:, t, :], in0=gates[:, 0:HID], in1=gates[:, HID:], op=ALU.mult
+                out=kept[:, t, :], in0=gates[:, 0, t, HID:], in1=c_masked[:, t, :], op=ALU.mult
             )
 
-        prepare_weights(2)
-        for first_tile in range(0, N_TILES, 2):
-            turn_state(s_sb, s_T, first_tile, nc.scalar.copy)
-
-        for t in range(N_TILES):
+        def after_output_and_candidate(t):
             m = mask_f32[:, t : t + 1]
-            pre = pre_activation(1, t)
-            gates = stage.tile([P, PAIR_COLS], F32)
-            nc.scalar.activation(out=gates[:], in_=pre[:], func=ACT.Sigmoid)
-            kept = stage.tile([P, HID], F32)
-            nc.gpsimd.tensor_tensor(out=kept[:], in0=gates[:, 0:HID], in1=c_tiles[:, t, :], op=ALU.mult)
-            cell = stage.tile([P, HID], F32)
-            nc.vector.tensor_tensor(out=cell[:], in0=kept[:], in1=in_term[:, t, :], op=ALU.add)
-            nc.scalar.activation(out=c_res[:, t, :], in_=cell[:], func=ACT.Copy, scale=m)
+            in_term = stage.tile([P, HID], F32)
+            nc.gpsimd.tensor_tensor(
+                out=in_term[:], in0=gates[:, 0, t, 0:HID], in1=gates[:, 1, t, HID:], op=ALU.mult
+            )
+            nc.vector.scalar_tensor_tensor(
+                out=c_res[:, t, :], in0=in_term[:], scalar=m, in1=kept[:, t, :], op0=ALU.mult, op1=ALU.add
+            )
             store(out_c, c_res, t)
             squashed = stage.tile([P, HID], F32)
-            nc.scalar.activation(out=squashed[:], in_=cell[:], func=ACT.Tanh, scale=m)
+            nc.scalar.activation(out=squashed[:], in_=c_res[:, t, :], func=ACT.Tanh)
             nc.scalar.activation(out=tanh_cell[:, t, :], in_=squashed[:], func=ACT.Copy, scale=m)
             nc.gpsimd.tensor_tensor(
-                out=h_res[:, t, :], in0=gates[:, HID:], in1=tanh_cell[:, t, :], op=ALU.mult
+                out=h_res[:, t, :], in0=gates[:, 1, t, 0:HID], in1=tanh_cell[:, t, :], op=ALU.mult
             )
             store(out_h, h_res, t)
 
-        for t in range(N_TILES):
-            pre = pre_activation(2, t)
-            gates = stage.tile([P, PAIR_COLS], F32)
-            nc.scalar.activation(out=gates[:], in_=pre[:], func=ACT.Sigmoid)
+        def after_share_gates(t):
             nc.gpsimd.tensor_tensor(
                 out=s_res[:, :, t, :],
-                in0=gates[:].rearrange("p (g n) -> p g n", g=2),
+                in0=gates[:, 2, t, :].rearrange("p (g n) -> p g n", g=2),
                 in1=tanh_cell[:, t, :].unsqueeze(1).to_broadcast([P, 2, HID]),
                 op=ALU.mult,
             )
             store(out_s0, s_res[:, 0, :, :], t)
             store(out_s1, s_res[:, 1, :, :], t)
+
+        prepare_gate(0, nc.scalar.copy, nc.vector.tensor_copy)
+        prepare_gate(1, nc.vector.tensor_copy, nc.scalar.copy)
+        prepare_inputs(0, nc.scalar.copy, nc.vector.tensor_copy)
+
+        nc.vector.tensor_copy(out=mask_f32[:], in_=mask_sb[:])
+        for t in range(N_TILES):
+            nc.gpsimd.tensor_scalar(
+                out=c_masked[:, t, :],
+                in0=c_sb[:, t, :],
+                scalar1=mask_f32[:, t : t + 1],
+                scalar2=0.0,
+                op0=ALU.mult,
+                op1=ALU.add,
+            )
+
+        jobs = [
+            lambda first=first: prepare_inputs(first, nc.scalar.copy, nc.scalar.copy)
+            for first in range(2, N_TILES, 2)
+        ]
+        jobs += [
+            lambda gate=gate: prepare_gate(gate, nc.scalar.copy, nc.scalar.copy)
+            for gate in range(2, N_GATES)
+        ]
+        jobs += [
+            lambda first=first: turn_state(s_sb, s_T, first, nc.scalar.copy)
+            for first in range(0, N_TILES, 2)
+        ]
+
+        for step in range(N_PAIRS * N_TILES):
+            if step < len(jobs):
+                jobs[step]()
+            pair, t = divmod(step, N_TILES)
+            gate_values(pair, t)
+            if pair == 0:
+                after_input_and_forget(t)
+            elif pair == 1:
+                after_output_and_candidate(t)
+            else:
+                after_share_gates(t)

@@ -23,8 +23,12 @@ N_GATES = 6
 N_PAIRS = N_GATES // 2
 N_RECURRENT = 4
 PAIR_COLS = 2 * HID
+GATE_TILES = N_GATES * HID // P
 PSUM_BANKS = 8
-STORE_TILES = 2
+SIDE = 4
+HALF_COLS = SIDE * P
+N_HALVES = N_TILES // SIDE
+GROUP = 2
 
 FLOPS = 2 * BATCH * (D_IN * N_GATES * HID + HID * N_GATES * HID)
 BYTES = (
@@ -58,20 +62,15 @@ def tile_share_lstm_cell_kernel(
     def by_batch_tile(dram):
         return dram.rearrange("(p t) n -> p t n", t=N_TILES)
 
-    def as_row(vector):
-        return vector.rearrange("(o n) -> o n", o=1)
-
     with ExitStack() as ctx:
         keep = ctx.enter_context(tc.tile_pool(name="keep", bufs=1))
-        stage = ctx.enter_context(tc.tile_pool(name="stage", bufs=4))
+        stage = ctx.enter_context(tc.tile_pool(name="stage", bufs=3))
         psum = ctx.enter_context(tc.psum_pool(name="psum", bufs=PSUM_BANKS))
 
         ident_f32 = keep.tile([P, P], F32)
         make_identity(nc, ident_f32[:])
         ident_bf16 = keep.tile([P, P], BF16)
         nc.vector.tensor_copy(out=ident_bf16[:], in_=ident_f32[:])
-        ones = keep.tile([P, P], BF16)
-        nc.vector.memset(ones[:], 1.0)
         warm = keep.tile([P, 1], F32)
         nc.vector.memset(warm[:], 0.0)
         nc.scalar.activation(out=warm[:], in_=warm[:], func=ACT.Sigmoid)
@@ -83,7 +82,7 @@ def tile_share_lstm_cell_kernel(
         w_in_sb = keep.tile([P, N_GATES * 2 * D_IN], BF16)
         w_rec_sb = keep.tile([P, N_GATES * 2 * HID], BF16)
         mask_sb = keep.tile([P, N_TILES], BF16)
-        bias_rows = keep.tile([P, N_GATES * HID], BF16)
+        bias_rows = keep.tile([P, P], BF16)
         nc.vector.memset(bias_rows[:], 0.0)
 
         def load_batch(tile_sb, dram, first, count):
@@ -112,25 +111,37 @@ def tile_share_lstm_cell_kernel(
                     share = gate - N_RECURRENT
                     load_gate(w_rec_sb, weight_sh[share * HID : (share + 1) * HID, :], gate)
 
-        nc.scalar.dma_start(out=bias_rows[0:1, :], in_=as_row(bias_ih))
-        nc.scalar.dma_start(out=bias_rows[1:2, 0 : N_RECURRENT * HID], in_=as_row(bias_hh))
-        nc.scalar.dma_start(out=bias_rows[1:2, N_RECURRENT * HID :], in_=as_row(bias_sh))
+        def as_rows(vector):
+            return vector.rearrange("(r n) -> r n", n=P)
+
+        rec_rows = N_RECURRENT * HID // P
+        nc.scalar.dma_start(out=bias_rows[0:GATE_TILES, :], in_=as_rows(bias_ih))
+        nc.scalar.dma_start(out=bias_rows[GATE_TILES : GATE_TILES + rec_rows, :], in_=as_rows(bias_hh))
+        nc.scalar.dma_start(out=bias_rows[GATE_TILES + rec_rows : 2 * GATE_TILES, :], in_=as_rows(bias_sh))
+        load_batch(x_sb, x, 0, SIDE)
         load_weights(0)
-        for first_tile in range(0, N_TILES, 2):
-            load_batch(x_sb, x, first_tile, 2)
-            load_batch(h_sb, h_minors, first_tile, 2)
+        load_batch(h_sb, h_minors, 0, SIDE)
+        load_batch(x_sb, x, SIDE, SIDE)
+        load_batch(h_sb, h_minors, SIDE, SIDE)
         load_weights(1)
         nc.sync.dma_start(out=mask_sb[:], in_=mask.rearrange("(p t) -> p t", t=N_TILES))
         nc.sync.dma_start(out=c_sb[:], in_=by_batch_tile(c_minors))
         load_weights(2)
         load_batch(s_sb, s_minors[idx, :, :], 0, N_TILES)
 
-        bias_all = keep.tile([P, N_GATES * HID], F32)
-        for pair in range(N_PAIRS):
-            cols = slice(pair * PAIR_COLS, (pair + 1) * PAIR_COLS)
-            spread = psum.tile([P, PAIR_COLS], F32, tag="bank")
-            nc.tensor.matmul(out=spread[:], lhsT=ones[:], rhs=bias_rows[:, cols], start=True, stop=True)
-            nc.vector.tensor_copy(out=bias_all[:, cols], in_=spread[:])
+        bias_col = keep.tile([P, GATE_TILES], F32)
+
+        def turn_biases():
+            bias_turned = psum.tile([P, P], BF16, tag="bank")
+            nc.tensor.transpose(bias_turned[:], bias_rows[:], ident_bf16[:])
+            bias_parts = keep.tile([P, 2 * GATE_TILES], F32)
+            nc.vector.tensor_copy(out=bias_parts[:], in_=bias_turned[:, 0 : 2 * GATE_TILES])
+            nc.vector.tensor_tensor(
+                out=bias_col[:], in0=bias_parts[:, 0:GATE_TILES], in1=bias_parts[:, GATE_TILES:], op=ALU.add
+            )
+
+        mask_f32 = keep.tile([P, N_TILES], F32)
+        nc.vector.tensor_copy(out=mask_f32[:], in_=mask_sb[:])
 
         x_codes = keep.tile([P, N_TILES * P], U32, align_bytes=64)
         x_scales = keep.tile([P, N_TILES * P], U8, align_bytes=64)
@@ -140,7 +151,7 @@ def tile_share_lstm_cell_kernel(
         s_T = keep.tile([P, N_TILES, HID], BF16)
         w_rec_T = keep.tile([P, N_PAIRS, K_CHUNKS, PAIR_COLS], BF16)
 
-        def quantise_two_blocks(source_sb, codes, scales, first_block, copy_out):
+        def quantise_two_blocks(source_sb, codes, scales, first_block):
             words = source_sb[:].bitcast(F32)
             turned = psum.tile([P, 2, 2, P], F32, tag="bank")
             for j in range(2):
@@ -148,7 +159,7 @@ def tile_share_lstm_cell_kernel(
                     first = (first_block + j) * WORDS + u * P
                     nc.tensor.transpose(turned[:, j, u, :], words[:, first : first + P], ident_f32[:])
             grouped = stage.tile([P, 2 * P * PACK], BF16, align_bytes=64)
-            copy_out(
+            nc.vector.tensor_copy(
                 out=grouped[:].bitcast(F32).rearrange("p (j r u) -> p j r u", j=2, u=2),
                 in_=turned[:].rearrange("p j u r -> p j r u"),
             )
@@ -157,155 +168,178 @@ def tile_share_lstm_cell_kernel(
                 out=codes[:, cols].bitcast(FP8X4), scales=scales[:, cols], in_=grouped[:]
             )
 
-        def turn_four_squares(squares, dest, copy_out):
+        def turn_four_squares(squares, dest):
             turned = psum.tile([P, 2, 2 * P], BF16, tag="bank")
             for i in range(4):
                 nc.tensor.transpose(
                     turned[:, i // 2, (i % 2) * P : (i % 2 + 1) * P], squares[i], ident_bf16[:]
                 )
-            copy_out(out=dest, in_=turned[:])
+            nc.vector.tensor_copy(out=dest, in_=turned[:])
 
-        def turn_state(state_sb, state_T, first_tile, copy_out):
+        def turn_state(state_sb, state_T, first_tile):
             squares = [
                 state_sb[:, (first_tile + j) * HID + c * P : (first_tile + j) * HID + (c + 1) * P]
                 for j in range(2)
                 for c in range(K_CHUNKS)
             ]
-            turn_four_squares(squares, state_T[:, first_tile : first_tile + 2, :], copy_out)
+            turn_four_squares(squares, state_T[:, first_tile : first_tile + 2, :])
 
-        def prepare_inputs(first_tile, copy_x, copy_h):
-            quantise_two_blocks(x_sb, x_codes, x_scales, first_tile, copy_x)
-            turn_state(h_sb, h_T, first_tile, copy_h)
-
-        def prepare_gate(gate, copy_in, copy_rec):
-            quantise_two_blocks(w_in_sb, w_codes, w_scales, 2 * gate, copy_in)
+        def turn_recurrent_weights(gate):
             squares = [
                 w_rec_sb[:, (2 * gate + r) * HID + c * P : (2 * gate + r) * HID + (c + 1) * P]
                 for c in range(K_CHUNKS)
                 for r in range(2)
             ]
             half = gate % 2
-            turn_four_squares(
-                squares, w_rec_T[:, gate // 2, :, half * HID : (half + 1) * HID], copy_rec
-            )
+            turn_four_squares(squares, w_rec_T[:, gate // 2, :, half * HID : (half + 1) * HID])
+
+        prepared = set()
+
+        def prepare_mx_operands(pair, half):
+            for first_tile in range(half * SIDE, (half + 1) * SIDE, 2):
+                if ("x", first_tile) not in prepared:
+                    prepared.add(("x", first_tile))
+                    quantise_two_blocks(x_sb, x_codes, x_scales, first_tile)
+            for gate in (2 * pair, 2 * pair + 1):
+                if ("w_in", gate) not in prepared:
+                    prepared.add(("w_in", gate))
+                    quantise_two_blocks(w_in_sb, w_codes, w_scales, 2 * gate)
+
+        def prepare_plain_operands(pair, half):
+            recurrent = 2 * pair < N_RECURRENT
+            for gate in (2 * pair, 2 * pair + 1):
+                if ("w_rec", gate) not in prepared:
+                    prepared.add(("w_rec", gate))
+                    turn_recurrent_weights(gate)
+            for first_tile in range(half * SIDE, (half + 1) * SIDE, 2):
+                if (recurrent, first_tile) not in prepared:
+                    prepared.add((recurrent, first_tile))
+                    if recurrent:
+                        turn_state(h_sb, h_T, first_tile)
+                    else:
+                        turn_state(s_sb, s_T, first_tile)
+
+        def mx_products(pair, half):
+            mx_T = stage.tile([P, SIDE, HALF_COLS], F32)
+            batch = slice(half * HALF_COLS, (half + 1) * HALF_COLS)
+            for j in range(SIDE):
+                gate_tile = SIDE * pair + j
+                rows = slice(gate_tile * P, (gate_tile + 1) * P)
+                acc_mx = psum.tile([P, HALF_COLS], F32, tag="bank")
+                nc.tensor.matmul_mx(
+                    out=acc_mx[:],
+                    lhsT=w_codes[:, rows].bitcast(FP8X4),
+                    lhsT_scale=w_scales[:, rows],
+                    rhs=x_codes[:, batch].bitcast(FP8X4),
+                    rhs_scale=x_scales[:, batch],
+                    start=True,
+                    stop=True,
+                )
+                nc.scalar.activation(
+                    out=mx_T[:, j, :],
+                    in_=acc_mx[:],
+                    func=ACT.Identity,
+                    bias=bias_col[:, gate_tile : gate_tile + 1],
+                )
+            return mx_T
 
         gates = keep.tile([P, N_PAIRS, N_TILES, PAIR_COLS], F32)
 
-        def gate_values(pair, t):
+        def gate_values(pair, t, mx_T):
             state_T = h_T if 2 * pair < N_RECURRENT else s_T
-            cols = slice(pair * PAIR_COLS, (pair + 1) * PAIR_COLS)
-            rows = slice(t * P, (t + 1) * P)
-            acc_plain = psum.tile([P, PAIR_COLS], F32, tag="bank")
+            pre = psum.tile([P, PAIR_COLS], F32, tag="bank")
             for c in range(K_CHUNKS):
                 nc.tensor.matmul(
-                    out=acc_plain[:],
+                    out=pre[:],
                     lhsT=state_T[:, t, c * P : (c + 1) * P],
                     rhs=w_rec_T[:, pair, c, :],
                     start=(c == 0),
-                    stop=(c == K_CHUNKS - 1),
+                    stop=False,
                 )
-            acc_mx = psum.tile([P, PAIR_COLS], F32, tag="bank")
-            nc.tensor.matmul_mx(
-                out=acc_mx[:],
-                lhsT=x_codes[:, rows].bitcast(FP8X4),
-                lhsT_scale=x_scales[:, rows],
-                rhs=w_codes[:, cols].bitcast(FP8X4),
-                rhs_scale=w_scales[:, cols],
-                start=True,
-                stop=True,
-            )
-            partial = stage.tile([P, PAIR_COLS], F32)
-            nc.vector.tensor_tensor(out=partial[:], in0=acc_plain[:], in1=bias_all[:, cols], op=ALU.add)
-            pre = stage.tile([P, PAIR_COLS], F32)
-            nc.vector.tensor_tensor(out=pre[:], in0=acc_mx[:], in1=partial[:], op=ALU.add)
+            q = t % SIDE
+            for j in range(SIDE):
+                nc.tensor.matmul(
+                    out=pre[:, j * P : (j + 1) * P],
+                    lhsT=mx_T[:, j, q * P : (q + 1) * P],
+                    rhs=ident_f32[:],
+                    is_transpose=True,
+                    start=False,
+                    stop=(j == SIDE - 1),
+                )
             if pair == 1:
                 nc.scalar.activation(out=gates[:, pair, t, 0:HID], in_=pre[:, 0:HID], func=ACT.Sigmoid)
                 nc.scalar.activation(out=gates[:, pair, t, HID:], in_=pre[:, HID:], func=ACT.Tanh)
             else:
                 nc.scalar.activation(out=gates[:, pair, t, :], in_=pre[:], func=ACT.Sigmoid)
 
-        def store(dram, result, t):
-            if t % STORE_TILES == STORE_TILES - 1:
-                group = slice(t + 1 - STORE_TILES, t + 1)
-                nc.sync.dma_start(out=by_batch_tile(dram)[:, group, :], in_=result[:, group, :])
-
-        mask_f32 = keep.tile([P, N_TILES], F32)
-        c_masked = keep.tile([P, N_TILES, HID], F32)
         kept = keep.tile([P, N_TILES, HID], F32)
-        tanh_cell = keep.tile([P, N_TILES, HID], F32)
+        squashed = keep.tile([P, N_TILES, HID], F32)
         h_res = keep.tile([P, N_TILES, HID], F32)
         c_res = keep.tile([P, N_TILES, HID], F32)
         s_res = keep.tile([P, 2, N_TILES, HID], F32)
 
+        def store(dram, result, t):
+            if t % GROUP == GROUP - 1:
+                group = slice(t + 1 - GROUP, t + 1)
+                nc.sync.dma_start(out=by_batch_tile(dram)[:, group, :], in_=result[:, group, :])
+
         def after_input_and_forget(t):
-            nc.gpsimd.tensor_tensor(
-                out=kept[:, t, :], in0=gates[:, 0, t, HID:], in1=c_masked[:, t, :], op=ALU.mult
+            nc.vector.tensor_tensor(
+                out=kept[:, t, :], in0=gates[:, 0, t, HID:], in1=c_sb[:, t, :], op=ALU.mult
             )
 
         def after_output_and_candidate(t):
             m = mask_f32[:, t : t + 1]
             in_term = stage.tile([P, HID], F32)
-            nc.gpsimd.tensor_tensor(
+            nc.vector.tensor_tensor(
                 out=in_term[:], in0=gates[:, 0, t, 0:HID], in1=gates[:, 1, t, HID:], op=ALU.mult
             )
-            nc.vector.scalar_tensor_tensor(
-                out=c_res[:, t, :], in0=in_term[:], scalar=m, in1=kept[:, t, :], op0=ALU.mult, op1=ALU.add
-            )
+            cell = stage.tile([P, HID], F32)
+            nc.vector.tensor_tensor(out=cell[:], in0=in_term[:], in1=kept[:, t, :], op=ALU.add)
+            nc.scalar.activation(out=squashed[:, t, :], in_=cell[:], func=ACT.Tanh, scale=m)
+            nc.vector.tensor_scalar_mul(out=c_res[:, t, :], in0=cell[:], scalar1=m)
             store(out_c, c_res, t)
-            squashed = stage.tile([P, HID], F32)
-            nc.scalar.activation(out=squashed[:], in_=c_res[:, t, :], func=ACT.Tanh)
-            nc.scalar.activation(out=tanh_cell[:, t, :], in_=squashed[:], func=ACT.Copy, scale=m)
-            nc.gpsimd.tensor_tensor(
-                out=h_res[:, t, :], in0=gates[:, 1, t, 0:HID], in1=tanh_cell[:, t, :], op=ALU.mult
+            nc.vector.scalar_tensor_tensor(
+                out=h_res[:, t, :],
+                in0=squashed[:, t, :],
+                scalar=m,
+                in1=gates[:, 1, t, 0:HID],
+                op0=ALU.mult,
+                op1=ALU.mult,
             )
             store(out_h, h_res, t)
 
         def after_share_gates(t):
-            nc.gpsimd.tensor_tensor(
-                out=s_res[:, :, t, :],
-                in0=gates[:, 2, t, :].rearrange("p (g n) -> p g n", g=2),
-                in1=tanh_cell[:, t, :].unsqueeze(1).to_broadcast([P, 2, HID]),
-                op=ALU.mult,
-            )
+            m = mask_f32[:, t : t + 1]
+            for share in range(2):
+                nc.vector.scalar_tensor_tensor(
+                    out=s_res[:, share, t, :],
+                    in0=squashed[:, t, :],
+                    scalar=m,
+                    in1=gates[:, 2, t, share * HID : (share + 1) * HID],
+                    op0=ALU.mult,
+                    op1=ALU.mult,
+                )
             store(out_s0, s_res[:, 0, :, :], t)
             store(out_s1, s_res[:, 1, :, :], t)
 
-        prepare_gate(0, nc.scalar.copy, nc.vector.tensor_copy)
-        prepare_gate(1, nc.vector.tensor_copy, nc.scalar.copy)
-        prepare_inputs(0, nc.scalar.copy, nc.vector.tensor_copy)
-
-        nc.vector.tensor_copy(out=mask_f32[:], in_=mask_sb[:])
-        for t in range(N_TILES):
-            nc.gpsimd.tensor_scalar(
-                out=c_masked[:, t, :],
-                in0=c_sb[:, t, :],
-                scalar1=mask_f32[:, t : t + 1],
-                scalar2=0.0,
-                op0=ALU.mult,
-                op1=ALU.add,
-            )
-
-        jobs = [
-            lambda first=first: prepare_inputs(first, nc.scalar.copy, nc.scalar.copy)
-            for first in range(2, N_TILES, 2)
-        ]
-        jobs += [
-            lambda gate=gate: prepare_gate(gate, nc.scalar.copy, nc.scalar.copy)
-            for gate in range(2, N_GATES)
-        ]
-        jobs += [
-            lambda first=first: turn_state(s_sb, s_T, first, nc.scalar.copy)
-            for first in range(0, N_TILES, 2)
-        ]
-
-        for step in range(N_PAIRS * N_TILES):
-            if step < len(jobs):
-                jobs[step]()
-            pair, t = divmod(step, N_TILES)
-            gate_values(pair, t)
-            if pair == 0:
-                after_input_and_forget(t)
-            elif pair == 1:
-                after_output_and_candidate(t)
-            else:
-                after_share_gates(t)
+        blocks = [(pair, half) for pair in range(N_PAIRS) for half in range(N_HALVES)]
+        prepare_mx_operands(*blocks[0])
+        turn_biases()
+        mx_T_next = mx_products(*blocks[0])
+        prepare_plain_operands(*blocks[0])
+        for k in range(len(blocks)):
+            pair, half = blocks[k]
+            mx_T = mx_T_next
+            if k + 1 < len(blocks):
+                prepare_mx_operands(*blocks[k + 1])
+                mx_T_next = mx_products(*blocks[k + 1])
+                prepare_plain_operands(*blocks[k + 1])
+            for t in range(half * SIDE, (half + 1) * SIDE):
+                gate_values(pair, t, mx_T)
+                if pair == 0:
+                    after_input_and_forget(t)
+                elif pair == 1:
+                    after_output_and_candidate(t)
+                else:
+                    after_share_gates(t)

@@ -29,6 +29,9 @@ SIDE = 4
 HALF_COLS = SIDE * P
 N_HALVES = N_TILES // SIDE
 GROUP = 2
+MX_AT = 2
+
+assert SIDE == 2 * K_CHUNKS
 
 FLOPS = 2 * BATCH * (D_IN * N_GATES * HID + HID * N_GATES * HID)
 BYTES = (
@@ -65,15 +68,16 @@ def tile_share_lstm_cell_kernel(
     with ExitStack() as ctx:
         keep = ctx.enter_context(tc.tile_pool(name="keep", bufs=1))
         stage = ctx.enter_context(tc.tile_pool(name="stage", bufs=3))
+        mx_pool = ctx.enter_context(tc.tile_pool(name="mx_pool", bufs=2))
         psum = ctx.enter_context(tc.psum_pool(name="psum", bufs=PSUM_BANKS))
+        ctx.enter_context(tc.manual_schedule())
 
+        bias_rows = keep.tile([P, P], BF16)
+        nc.gpsimd.memset(bias_rows[:], 0.0)
         ident_f32 = keep.tile([P, P], F32)
         make_identity(nc, ident_f32[:])
         ident_bf16 = keep.tile([P, P], BF16)
         nc.vector.tensor_copy(out=ident_bf16[:], in_=ident_f32[:])
-        warm = keep.tile([P, 1], F32)
-        nc.vector.memset(warm[:], 0.0)
-        nc.scalar.activation(out=warm[:], in_=warm[:], func=ACT.Sigmoid)
 
         x_sb = keep.tile([P, N_TILES * D_IN], BF16)
         h_sb = keep.tile([P, N_TILES * HID], BF16)
@@ -82,8 +86,6 @@ def tile_share_lstm_cell_kernel(
         w_in_sb = keep.tile([P, N_GATES * 2 * D_IN], BF16)
         w_rec_sb = keep.tile([P, N_GATES * 2 * HID], BF16)
         mask_sb = keep.tile([P, N_TILES], BF16)
-        bias_rows = keep.tile([P, P], BF16)
-        nc.vector.memset(bias_rows[:], 0.0)
 
         def load_batch(tile_sb, dram, first, count):
             view = tile_sb[:].rearrange("p (t n) -> p t n", t=N_TILES)
@@ -101,32 +103,45 @@ def tile_share_lstm_cell_kernel(
                 in_=rows.rearrange("(r p) n -> p r n", p=P),
             )
 
-        def load_weights(pair):
-            for gate in (2 * pair, 2 * pair + 1):
-                load_gate(w_in_sb, weight_ih[gate * HID : (gate + 1) * HID, :], gate)
-            for gate in (2 * pair, 2 * pair + 1):
-                if gate < N_RECURRENT:
-                    load_gate(w_rec_sb, weight_hh[gate * HID : (gate + 1) * HID, :], gate)
-                else:
-                    share = gate - N_RECURRENT
-                    load_gate(w_rec_sb, weight_sh[share * HID : (share + 1) * HID, :], gate)
+        def load_in_weights(gate):
+            load_gate(w_in_sb, weight_ih[gate * HID : (gate + 1) * HID, :], gate)
+
+        def load_recurrent_weights(gate):
+            if gate < N_RECURRENT:
+                load_gate(w_rec_sb, weight_hh[gate * HID : (gate + 1) * HID, :], gate)
+            else:
+                share = gate - N_RECURRENT
+                load_gate(w_rec_sb, weight_sh[share * HID : (share + 1) * HID, :], gate)
 
         def as_rows(vector):
             return vector.rearrange("(r n) -> r n", n=P)
 
         rec_rows = N_RECURRENT * HID // P
-        nc.scalar.dma_start(out=bias_rows[0:GATE_TILES, :], in_=as_rows(bias_ih))
-        nc.scalar.dma_start(out=bias_rows[GATE_TILES : GATE_TILES + rec_rows, :], in_=as_rows(bias_hh))
-        nc.scalar.dma_start(out=bias_rows[GATE_TILES + rec_rows : 2 * GATE_TILES, :], in_=as_rows(bias_sh))
-        load_batch(x_sb, x, 0, SIDE)
-        load_weights(0)
+        nc.sync.dma_start(out=bias_rows[0:GATE_TILES, :], in_=as_rows(bias_ih))
+        nc.sync.dma_start(out=bias_rows[GATE_TILES : GATE_TILES + rec_rows, :], in_=as_rows(bias_hh))
+        nc.sync.dma_start(out=bias_rows[GATE_TILES + rec_rows : 2 * GATE_TILES, :], in_=as_rows(bias_sh))
+        warm = keep.tile([P, 1], F32)
+        nc.vector.memset(warm[:], 0.0)
+        nc.scalar.activation(out=warm[:], in_=warm[:], func=ACT.Sigmoid)
+        load_in_weights(0)
+        load_batch(x_sb, x, 0, 2)
+        load_batch(x_sb, x, 2, 2)
+        load_in_weights(1)
+        load_recurrent_weights(0)
+        load_recurrent_weights(1)
         load_batch(h_sb, h_minors, 0, SIDE)
         load_batch(x_sb, x, SIDE, SIDE)
+        load_in_weights(2)
+        load_in_weights(3)
         load_batch(h_sb, h_minors, SIDE, SIDE)
-        load_weights(1)
+        load_recurrent_weights(2)
+        load_recurrent_weights(3)
         nc.sync.dma_start(out=mask_sb[:], in_=mask.rearrange("(p t) -> p t", t=N_TILES))
         nc.sync.dma_start(out=c_sb[:], in_=by_batch_tile(c_minors))
-        load_weights(2)
+        load_in_weights(4)
+        load_in_weights(5)
+        load_recurrent_weights(4)
+        load_recurrent_weights(5)
         load_batch(s_sb, s_minors[idx, :, :], 0, N_TILES)
 
         bias_col = keep.tile([P, GATE_TILES], F32)
@@ -141,7 +156,7 @@ def tile_share_lstm_cell_kernel(
             )
 
         mask_f32 = keep.tile([P, N_TILES], F32)
-        nc.vector.tensor_copy(out=mask_f32[:], in_=mask_sb[:])
+        nc.gpsimd.tensor_copy(out=mask_f32[:], in_=mask_sb[:])
 
         x_codes = keep.tile([P, N_TILES * P], U32, align_bytes=64)
         x_scales = keep.tile([P, N_TILES * P], U8, align_bytes=64)
@@ -151,7 +166,7 @@ def tile_share_lstm_cell_kernel(
         s_T = keep.tile([P, N_TILES, HID], BF16)
         w_rec_T = keep.tile([P, N_PAIRS, K_CHUNKS, PAIR_COLS], BF16)
 
-        def quantise_two_blocks(source_sb, codes, scales, first_block):
+        def turn_two_blocks(source_sb, first_block, copy_out):
             words = source_sb[:].bitcast(F32)
             turned = psum.tile([P, 2, 2, P], F32, tag="bank")
             for j in range(2):
@@ -159,10 +174,13 @@ def tile_share_lstm_cell_kernel(
                     first = (first_block + j) * WORDS + u * P
                     nc.tensor.transpose(turned[:, j, u, :], words[:, first : first + P], ident_f32[:])
             grouped = stage.tile([P, 2 * P * PACK], BF16, align_bytes=64)
-            nc.vector.tensor_copy(
+            copy_out(
                 out=grouped[:].bitcast(F32).rearrange("p (j r u) -> p j r u", j=2, u=2),
                 in_=turned[:].rearrange("p j u r -> p j r u"),
             )
+            return grouped
+
+        def quantise_two_blocks(grouped, codes, scales, first_block):
             cols = slice(first_block * P, (first_block + 2) * P)
             nc.vector.quantize_mx(
                 out=codes[:, cols].bitcast(FP8X4), scales=scales[:, cols], in_=grouped[:]
@@ -174,7 +192,7 @@ def tile_share_lstm_cell_kernel(
                 nc.tensor.transpose(
                     turned[:, i // 2, (i % 2) * P : (i % 2 + 1) * P], squares[i], ident_bf16[:]
                 )
-            nc.vector.tensor_copy(out=dest, in_=turned[:])
+            nc.scalar.copy(out=dest, in_=turned[:])
 
         def turn_state(state_sb, state_T, first_tile):
             squares = [
@@ -193,35 +211,10 @@ def tile_share_lstm_cell_kernel(
             half = gate % 2
             turn_four_squares(squares, w_rec_T[:, gate // 2, :, half * HID : (half + 1) * HID])
 
-        prepared = set()
-
-        def prepare_mx_operands(pair, half):
-            for first_tile in range(half * SIDE, (half + 1) * SIDE, 2):
-                if ("x", first_tile) not in prepared:
-                    prepared.add(("x", first_tile))
-                    quantise_two_blocks(x_sb, x_codes, x_scales, first_tile)
-            for gate in (2 * pair, 2 * pair + 1):
-                if ("w_in", gate) not in prepared:
-                    prepared.add(("w_in", gate))
-                    quantise_two_blocks(w_in_sb, w_codes, w_scales, 2 * gate)
-
-        def prepare_plain_operands(pair, half):
-            recurrent = 2 * pair < N_RECURRENT
-            for gate in (2 * pair, 2 * pair + 1):
-                if ("w_rec", gate) not in prepared:
-                    prepared.add(("w_rec", gate))
-                    turn_recurrent_weights(gate)
-            for first_tile in range(half * SIDE, (half + 1) * SIDE, 2):
-                if (recurrent, first_tile) not in prepared:
-                    prepared.add((recurrent, first_tile))
-                    if recurrent:
-                        turn_state(h_sb, h_T, first_tile)
-                    else:
-                        turn_state(s_sb, s_T, first_tile)
-
         def mx_products(pair, half):
-            mx_T = stage.tile([P, SIDE, HALF_COLS], F32)
+            mx_T = mx_pool.tile([P, SIDE, HALF_COLS], F32)
             batch = slice(half * HALF_COLS, (half + 1) * HALF_COLS)
+            banks = []
             for j in range(SIDE):
                 gate_tile = SIDE * pair + j
                 rows = slice(gate_tile * P, (gate_tile + 1) * P)
@@ -235,37 +228,51 @@ def tile_share_lstm_cell_kernel(
                     start=True,
                     stop=True,
                 )
-                nc.scalar.activation(
-                    out=mx_T[:, j, :],
-                    in_=acc_mx[:],
-                    func=ACT.Identity,
-                    bias=bias_col[:, gate_tile : gate_tile + 1],
-                )
+                banks.append(acc_mx)
+            for j in range(SIDE):
+                bias = bias_col[:, SIDE * pair + j : SIDE * pair + j + 1]
+                if j % 2 == 0:
+                    nc.scalar.activation(out=mx_T[:, j, :], in_=banks[j][:], func=ACT.Identity, bias=bias)
+                else:
+                    nc.vector.tensor_scalar_add(out=mx_T[:, j, :], in0=banks[j][:], scalar1=bias)
             return mx_T
 
+        steps = [
+            (pair, half * SIDE + q)
+            for pair in range(N_PAIRS)
+            for half in range(N_HALVES)
+            for q in range(SIDE)
+        ]
         gates = keep.tile([P, N_PAIRS, N_TILES, PAIR_COLS], F32)
+        mx_T_of = {}
+        pre_of = {}
 
-        def gate_values(pair, t, mx_T):
+        def plain_pass(pair, t, c):
+            if c == 0:
+                bank = psum.tile([P, PAIR_COLS], F32, tag="bank")
+                pre_of[(pair, t)] = bank
             state_T = h_T if 2 * pair < N_RECURRENT else s_T
-            pre = psum.tile([P, PAIR_COLS], F32, tag="bank")
-            for c in range(K_CHUNKS):
-                nc.tensor.matmul(
-                    out=pre[:],
-                    lhsT=state_T[:, t, c * P : (c + 1) * P],
-                    rhs=w_rec_T[:, pair, c, :],
-                    start=(c == 0),
-                    stop=False,
-                )
+            nc.tensor.matmul(
+                out=pre_of[(pair, t)][:],
+                lhsT=state_T[:, t, c * P : (c + 1) * P],
+                rhs=w_rec_T[:, pair, c, :],
+                start=(c == 0),
+                stop=False,
+            )
+
+        def add_mx_product(pair, t, j):
             q = t % SIDE
-            for j in range(SIDE):
-                nc.tensor.matmul(
-                    out=pre[:, j * P : (j + 1) * P],
-                    lhsT=mx_T[:, j, q * P : (q + 1) * P],
-                    rhs=ident_f32[:],
-                    is_transpose=True,
-                    start=False,
-                    stop=(j == SIDE - 1),
-                )
+            nc.tensor.matmul(
+                out=pre_of[(pair, t)][:, j * P : (j + 1) * P],
+                lhsT=mx_T_of[(pair, t // SIDE)][:, j, q * P : (q + 1) * P],
+                rhs=ident_f32[:],
+                is_transpose=True,
+                start=False,
+                stop=(j == SIDE - 1),
+            )
+
+        def activations(pair, t):
+            pre = pre_of[(pair, t)]
             if pair == 1:
                 nc.scalar.activation(out=gates[:, pair, t, 0:HID], in_=pre[:, 0:HID], func=ACT.Sigmoid)
                 nc.scalar.activation(out=gates[:, pair, t, HID:], in_=pre[:, HID:], func=ACT.Tanh)
@@ -273,6 +280,7 @@ def tile_share_lstm_cell_kernel(
                 nc.scalar.activation(out=gates[:, pair, t, :], in_=pre[:], func=ACT.Sigmoid)
 
         kept = keep.tile([P, N_TILES, HID], F32)
+        cell = keep.tile([P, N_TILES, HID], F32)
         squashed = keep.tile([P, N_TILES, HID], F32)
         h_res = keep.tile([P, N_TILES, HID], F32)
         c_res = keep.tile([P, N_TILES, HID], F32)
@@ -283,63 +291,100 @@ def tile_share_lstm_cell_kernel(
                 group = slice(t + 1 - GROUP, t + 1)
                 nc.sync.dma_start(out=by_batch_tile(dram)[:, group, :], in_=result[:, group, :])
 
-        def after_input_and_forget(t):
-            nc.vector.tensor_tensor(
-                out=kept[:, t, :], in0=gates[:, 0, t, HID:], in1=c_sb[:, t, :], op=ALU.mult
-            )
-
-        def after_output_and_candidate(t):
-            m = mask_f32[:, t : t + 1]
-            in_term = stage.tile([P, HID], F32)
-            nc.vector.tensor_tensor(
-                out=in_term[:], in0=gates[:, 0, t, 0:HID], in1=gates[:, 1, t, HID:], op=ALU.mult
-            )
-            cell = stage.tile([P, HID], F32)
-            nc.vector.tensor_tensor(out=cell[:], in0=in_term[:], in1=kept[:, t, :], op=ALU.add)
-            nc.scalar.activation(out=squashed[:, t, :], in_=cell[:], func=ACT.Tanh, scale=m)
-            nc.vector.tensor_scalar_mul(out=c_res[:, t, :], in0=cell[:], scalar1=m)
-            store(out_c, c_res, t)
+        def times_masked_tanh(out, gate, t):
             nc.vector.scalar_tensor_tensor(
-                out=h_res[:, t, :],
+                out=out,
                 in0=squashed[:, t, :],
-                scalar=m,
-                in1=gates[:, 1, t, 0:HID],
+                scalar=mask_f32[:, t : t + 1],
+                in1=gate,
                 op0=ALU.mult,
                 op1=ALU.mult,
             )
-            store(out_h, h_res, t)
 
-        def after_share_gates(t):
-            m = mask_f32[:, t : t + 1]
-            for share in range(2):
-                nc.vector.scalar_tensor_tensor(
-                    out=s_res[:, share, t, :],
-                    in0=squashed[:, t, :],
-                    scalar=m,
-                    in1=gates[:, 2, t, share * HID : (share + 1) * HID],
-                    op0=ALU.mult,
-                    op1=ALU.mult,
+        def products(pair, t):
+            if pair == 0:
+                nc.vector.tensor_tensor(
+                    out=kept[:, t, :], in0=gates[:, 0, t, HID:], in1=c_sb[:, t, :], op=ALU.mult
                 )
-            store(out_s0, s_res[:, 0, :, :], t)
-            store(out_s1, s_res[:, 1, :, :], t)
+            elif pair == 1:
+                in_term = stage.tile([P, HID], F32)
+                nc.vector.tensor_tensor(
+                    out=in_term[:], in0=gates[:, 0, t, 0:HID], in1=gates[:, 1, t, HID:], op=ALU.mult
+                )
+                nc.vector.tensor_tensor(out=cell[:, t, :], in0=in_term[:], in1=kept[:, t, :], op=ALU.add)
+            else:
+                for share in range(2):
+                    times_masked_tanh(s_res[:, share, t, :], gates[:, 2, t, share * HID : (share + 1) * HID], t)
+                store(out_s0, s_res[:, 0, :, :], t)
+                store(out_s1, s_res[:, 1, :, :], t)
 
-        blocks = [(pair, half) for pair in range(N_PAIRS) for half in range(N_HALVES)]
-        prepare_mx_operands(*blocks[0])
+        def new_cell(pair, t):
+            if pair == 1:
+                m = mask_f32[:, t : t + 1]
+                nc.scalar.activation(out=squashed[:, t, :], in_=cell[:, t, :], func=ACT.Tanh, scale=m)
+                nc.vector.tensor_scalar_mul(out=c_res[:, t, :], in0=cell[:, t, :], scalar1=m)
+                store(out_c, c_res, t)
+
+        def new_hidden(pair, t):
+            if pair == 1:
+                times_masked_tanh(h_res[:, t, :], gates[:, 1, t, 0:HID], t)
+                store(out_h, h_res, t)
+
+        first_w = turn_two_blocks(w_in_sb, 0, nc.vector.tensor_copy)
+        first_x = turn_two_blocks(x_sb, 0, nc.scalar.copy)
+        second_x = turn_two_blocks(x_sb, 2, nc.vector.tensor_copy)
+        quantise_two_blocks(first_w, w_codes, w_scales, 0)
+        second_w = turn_two_blocks(w_in_sb, 2, nc.scalar.copy)
+        quantise_two_blocks(first_x, x_codes, x_scales, 0)
+        quantise_two_blocks(second_x, x_codes, x_scales, 2)
         turn_biases()
-        mx_T_next = mx_products(*blocks[0])
-        prepare_plain_operands(*blocks[0])
-        for k in range(len(blocks)):
-            pair, half = blocks[k]
-            mx_T = mx_T_next
-            if k + 1 < len(blocks):
-                prepare_mx_operands(*blocks[k + 1])
-                mx_T_next = mx_products(*blocks[k + 1])
-                prepare_plain_operands(*blocks[k + 1])
-            for t in range(half * SIDE, (half + 1) * SIDE):
-                gate_values(pair, t, mx_T)
-                if pair == 0:
-                    after_input_and_forget(t)
-                elif pair == 1:
-                    after_output_and_candidate(t)
-                else:
-                    after_share_gates(t)
+        quantise_two_blocks(second_w, w_codes, w_scales, 2)
+        mx_T_of[(0, 0)] = mx_products(0, 0)
+        turn_recurrent_weights(0)
+        turn_recurrent_weights(1)
+        turn_state(h_sb, h_T, 0)
+        turn_state(h_sb, h_T, 2)
+        third_x = turn_two_blocks(x_sb, 4, nc.vector.tensor_copy)
+        fourth_x = turn_two_blocks(x_sb, 6, nc.scalar.copy)
+        quantise_two_blocks(third_x, x_codes, x_scales, 4)
+        quantise_two_blocks(fourth_x, x_codes, x_scales, 6)
+
+        waiting = []
+
+        def prepare_in_weights(gate):
+            grouped = turn_two_blocks(w_in_sb, 2 * gate, nc.vector.tensor_copy)
+            waiting.append(lambda: quantise_two_blocks(grouped, w_codes, w_scales, 2 * gate))
+
+        jobs = [lambda gate=gate: prepare_in_weights(gate) for gate in (2, 3)]
+        jobs += [lambda first=first: turn_state(h_sb, h_T, first) for first in (4, 6)]
+        jobs += [lambda gate=gate: turn_recurrent_weights(gate) for gate in (2, 3)]
+        jobs += [lambda gate=gate: prepare_in_weights(gate) for gate in (4, 5)]
+        jobs += [lambda gate=gate: turn_recurrent_weights(gate) for gate in (4, 5)]
+        jobs += [lambda first=first: turn_state(s_sb, s_T, first) for first in range(0, N_TILES, 2)]
+
+        def lagged(stage_of_step, n, lag):
+            if 0 <= n - lag < len(steps):
+                stage_of_step(*steps[n - lag])
+
+        for c in range(K_CHUNKS):
+            plain_pass(*steps[0], c)
+        for n in range(len(steps) + 4):
+            if n < len(steps):
+                pair, t = steps[n]
+                block = n // SIDE
+                if n % SIDE == MX_AT and block + 1 < N_PAIRS * N_HALVES:
+                    ahead = divmod(block + 1, N_HALVES)
+                    mx_T_of[ahead] = mx_products(*ahead)
+                for c in range(K_CHUNKS):
+                    if n + 1 < len(steps):
+                        plain_pass(*steps[n + 1], c)
+                    add_mx_product(pair, t, 2 * c)
+                    add_mx_product(pair, t, 2 * c + 1)
+                while waiting:
+                    waiting.pop(0)()
+                if n < len(jobs):
+                    jobs[n]()
+            lagged(activations, n, 1)
+            lagged(products, n, 2)
+            lagged(new_cell, n, 3)
+            lagged(new_hidden, n, 4)

@@ -28,7 +28,6 @@ PSUM_BANKS = 8
 SIDE = 4
 HALF_COLS = SIDE * P
 N_HALVES = N_TILES // SIDE
-GROUP = 2
 MX_AT = 2
 
 assert SIDE == 2 * K_CHUNKS
@@ -117,9 +116,6 @@ def tile_share_lstm_cell_kernel(
             return vector.rearrange("(r n) -> r n", n=P)
 
         rec_rows = N_RECURRENT * HID // P
-        nc.sync.dma_start(out=bias_rows[0:GATE_TILES, :], in_=as_rows(bias_ih))
-        nc.sync.dma_start(out=bias_rows[GATE_TILES : GATE_TILES + rec_rows, :], in_=as_rows(bias_hh))
-        nc.sync.dma_start(out=bias_rows[GATE_TILES + rec_rows : 2 * GATE_TILES, :], in_=as_rows(bias_sh))
         warm = keep.tile([P, 1], F32)
         nc.vector.memset(warm[:], 0.0)
         nc.scalar.activation(out=warm[:], in_=warm[:], func=ACT.Sigmoid)
@@ -127,6 +123,9 @@ def tile_share_lstm_cell_kernel(
         load_batch(x_sb, x, 0, 2)
         load_batch(x_sb, x, 2, 2)
         load_in_weights(1)
+        nc.sync.dma_start(out=bias_rows[0:GATE_TILES, :], in_=as_rows(bias_ih))
+        nc.sync.dma_start(out=bias_rows[GATE_TILES : GATE_TILES + rec_rows, :], in_=as_rows(bias_hh))
+        nc.sync.dma_start(out=bias_rows[GATE_TILES + rec_rows : 2 * GATE_TILES, :], in_=as_rows(bias_sh))
         load_recurrent_weights(0)
         load_recurrent_weights(1)
         load_batch(h_sb, h_minors, 0, SIDE)
@@ -162,9 +161,12 @@ def tile_share_lstm_cell_kernel(
         x_scales = keep.tile([P, N_TILES * P], U8, align_bytes=64)
         w_codes = keep.tile([P, N_GATES * HID], U32, align_bytes=64)
         w_scales = keep.tile([P, N_GATES * HID], U8, align_bytes=64)
-        h_T = keep.tile([P, N_TILES, HID], BF16)
-        s_T = keep.tile([P, N_TILES, HID], BF16)
-        w_rec_T = keep.tile([P, N_PAIRS, K_CHUNKS, PAIR_COLS], BF16)
+        h_T_words = keep.tile([P, N_TILES * P], F32)
+        s_T_words = keep.tile([P, N_TILES * P], F32)
+        w_rec_T_words = keep.tile([P, N_PAIRS * PAIR_COLS], F32)
+        h_T = h_T_words[:].bitcast(BF16).rearrange("p (t b e) -> p t b e", t=N_TILES, e=2)
+        s_T = s_T_words[:].bitcast(BF16).rearrange("p (t b e) -> p t b e", t=N_TILES, e=2)
+        w_rec_T = w_rec_T_words[:].bitcast(BF16).rearrange("p (g n e) -> p g n e", g=N_PAIRS, e=2)
 
         def turn_two_blocks(source_sb, first_block, copy_out):
             words = source_sb[:].bitcast(F32)
@@ -186,30 +188,13 @@ def tile_share_lstm_cell_kernel(
                 out=codes[:, cols].bitcast(FP8X4), scales=scales[:, cols], in_=grouped[:]
             )
 
-        def turn_four_squares(squares, dest):
-            turned = psum.tile([P, 2, 2 * P], BF16, tag="bank")
-            for i in range(4):
-                nc.tensor.transpose(
-                    turned[:, i // 2, (i % 2) * P : (i % 2 + 1) * P], squares[i], ident_bf16[:]
-                )
-            nc.scalar.copy(out=dest, in_=turned[:])
-
-        def turn_state(state_sb, state_T, first_tile):
-            squares = [
-                state_sb[:, (first_tile + j) * HID + c * P : (first_tile + j) * HID + (c + 1) * P]
-                for j in range(2)
-                for c in range(K_CHUNKS)
-            ]
-            turn_four_squares(squares, state_T[:, first_tile : first_tile + 2, :])
-
-        def turn_recurrent_weights(gate):
-            squares = [
-                w_rec_sb[:, (2 * gate + r) * HID + c * P : (2 * gate + r) * HID + (c + 1) * P]
-                for c in range(K_CHUNKS)
-                for r in range(2)
-            ]
-            half = gate % 2
-            turn_four_squares(squares, w_rec_T[:, gate // 2, :, half * HID : (half + 1) * HID])
+        def turn_four_blocks(source_sb, dest_words, first_block, copy_out):
+            words = source_sb[:].bitcast(F32)
+            turned = psum.tile([P, SIDE * P], F32, tag="bank")
+            for i in range(SIDE):
+                cols = slice((first_block + i) * P, (first_block + i + 1) * P)
+                nc.tensor.transpose(turned[:, i * P : (i + 1) * P], words[:, cols], ident_f32[:])
+            copy_out(out=dest_words[:, first_block * P : (first_block + SIDE) * P], in_=turned[:])
 
         def mx_products(pair, half):
             mx_T = mx_pool.tile([P, SIDE, HALF_COLS], F32)
@@ -254,8 +239,8 @@ def tile_share_lstm_cell_kernel(
             state_T = h_T if 2 * pair < N_RECURRENT else s_T
             nc.tensor.matmul(
                 out=pre_of[(pair, t)][:],
-                lhsT=state_T[:, t, c * P : (c + 1) * P],
-                rhs=w_rec_T[:, pair, c, :],
+                lhsT=state_T[:, t, :, c],
+                rhs=w_rec_T[:, pair, :, c],
                 start=(c == 0),
                 stop=False,
             )
@@ -287,9 +272,7 @@ def tile_share_lstm_cell_kernel(
         s_res = keep.tile([P, 2, N_TILES, HID], F32)
 
         def store(dram, result, t):
-            if t % GROUP == GROUP - 1:
-                group = slice(t + 1 - GROUP, t + 1)
-                nc.sync.dma_start(out=by_batch_tile(dram)[:, group, :], in_=result[:, group, :])
+            nc.sync.dma_start(out=by_batch_tile(dram)[:, t, :], in_=result[:, t, :])
 
         def times_masked_tanh(out, gate, t):
             nc.vector.scalar_tensor_tensor(
@@ -337,13 +320,11 @@ def tile_share_lstm_cell_kernel(
         second_w = turn_two_blocks(w_in_sb, 2, nc.scalar.copy)
         quantise_two_blocks(first_x, x_codes, x_scales, 0)
         quantise_two_blocks(second_x, x_codes, x_scales, 2)
+        turn_four_blocks(w_rec_sb, w_rec_T_words, 0, nc.scalar.copy)
+        turn_four_blocks(h_sb, h_T_words, 0, nc.vector.tensor_copy)
         turn_biases()
         quantise_two_blocks(second_w, w_codes, w_scales, 2)
         mx_T_of[(0, 0)] = mx_products(0, 0)
-        turn_recurrent_weights(0)
-        turn_recurrent_weights(1)
-        turn_state(h_sb, h_T, 0)
-        turn_state(h_sb, h_T, 2)
         third_x = turn_two_blocks(x_sb, 4, nc.vector.tensor_copy)
         fourth_x = turn_two_blocks(x_sb, 6, nc.scalar.copy)
         quantise_two_blocks(third_x, x_codes, x_scales, 4)
@@ -356,11 +337,12 @@ def tile_share_lstm_cell_kernel(
             waiting.append(lambda: quantise_two_blocks(grouped, w_codes, w_scales, 2 * gate))
 
         jobs = [lambda gate=gate: prepare_in_weights(gate) for gate in (2, 3)]
-        jobs += [lambda first=first: turn_state(h_sb, h_T, first) for first in (4, 6)]
-        jobs += [lambda gate=gate: turn_recurrent_weights(gate) for gate in (2, 3)]
+        jobs.append(lambda: turn_four_blocks(h_sb, h_T_words, SIDE, nc.scalar.copy))
+        jobs.append(lambda: turn_four_blocks(w_rec_sb, w_rec_T_words, SIDE, nc.scalar.copy))
         jobs += [lambda gate=gate: prepare_in_weights(gate) for gate in (4, 5)]
-        jobs += [lambda gate=gate: turn_recurrent_weights(gate) for gate in (4, 5)]
-        jobs += [lambda first=first: turn_state(s_sb, s_T, first) for first in range(0, N_TILES, 2)]
+        jobs.append(lambda: turn_four_blocks(w_rec_sb, w_rec_T_words, 2 * SIDE, nc.scalar.copy))
+        jobs.append(lambda: turn_four_blocks(s_sb, s_T_words, 0, nc.scalar.copy))
+        jobs.append(lambda: turn_four_blocks(s_sb, s_T_words, SIDE, nc.scalar.copy))
 
         def lagged(stage_of_step, n, lag):
             if 0 <= n - lag < len(steps):

@@ -28,7 +28,7 @@ PSUM_BANKS = 8
 SIDE = 4
 HALF_COLS = SIDE * P
 N_HALVES = N_TILES // SIDE
-MX_AT = 2
+MX_AT = 3
 
 assert SIDE == 2 * K_CHUNKS
 

@@ -337,12 +337,12 @@ def tile_share_lstm_cell_kernel(
             waiting.append(lambda: quantise_two_blocks(grouped, w_codes, w_scales, 2 * gate))
 
         jobs = [lambda gate=gate: prepare_in_weights(gate) for gate in (2, 3)]
-        jobs.append(lambda: turn_four_blocks(h_sb, h_T_words, SIDE, nc.scalar.copy))
-        jobs.append(lambda: turn_four_blocks(w_rec_sb, w_rec_T_words, SIDE, nc.scalar.copy))
+        jobs.append(lambda: turn_four_blocks(h_sb, h_T_words, SIDE, nc.vector.tensor_copy))
+        jobs.append(lambda: turn_four_blocks(w_rec_sb, w_rec_T_words, SIDE, nc.vector.tensor_copy))
         jobs += [lambda gate=gate: prepare_in_weights(gate) for gate in (4, 5)]
-        jobs.append(lambda: turn_four_blocks(w_rec_sb, w_rec_T_words, 2 * SIDE, nc.scalar.copy))
-        jobs.append(lambda: turn_four_blocks(s_sb, s_T_words, 0, nc.scalar.copy))
-        jobs.append(lambda: turn_four_blocks(s_sb, s_T_words, SIDE, nc.scalar.copy))
+        jobs.append(lambda: turn_four_blocks(w_rec_sb, w_rec_T_words, 2 * SIDE, nc.vector.tensor_copy))
+        jobs.append(lambda: turn_four_blocks(s_sb, s_T_words, 0, nc.vector.tensor_copy))
+        jobs.append(lambda: turn_four_blocks(s_sb, s_T_words, SIDE, nc.vector.tensor_copy))
 
         def lagged(stage_of_step, n, lag):
             if 0 <= n - lag < len(steps):

from contextlib import ExitStack

import concourse.mybir as mybir
from concourse.masks import make_identity

FP8X4 = mybir.dt.float8_e4m3fn_x4
BF16 = mybir.dt.bfloat16
F32 = mybir.dt.float32
U32 = mybir.dt.uint32
U8 = mybir.dt.uint8
ACT = mybir.ActivationFunctionType
ALU = mybir.AluOpType

P = 128
PACK = 4
BATCH = 1024
D_IN = 512
HID = 256
N_TILES = BATCH // P
WORDS = D_IN // 2
K_CHUNKS = HID // P
N_GATES = 6
N_PAIRS = N_GATES // 2
N_RECURRENT = 4
PAIR_COLS = 2 * HID
GATE_TILES = N_GATES * HID // P
PSUM_BANKS = 8
SIDE = 4
HALF_COLS = SIDE * P
N_HALVES = N_TILES // SIDE
MX_AT = 3

assert SIDE == 2 * K_CHUNKS

FLOPS = 2 * BATCH * (D_IN * N_GATES * HID + HID * N_GATES * HID)
BYTES = (
    2 * (BATCH * D_IN + 3 * BATCH * HID + BATCH)
    + 2 * (N_GATES * HID * (D_IN + HID) + 2 * N_GATES * HID)
    + 4 * 4 * BATCH * HID
)


def tile_share_lstm_cell_kernel(
    tc,
    x,
    h_minors,
    c_minors,
    s_minors,
    mask,
    weight_ih,
    weight_hh,
    weight_sh,
    bias_ih,
    bias_hh,
    bias_sh,
    idx,
    out_h,
    out_c,
    out_s0,
    out_s1,
):
    nc = tc.nc

    def by_batch_tile(dram):
        return dram.rearrange("(p t) n -> p t n", t=N_TILES)

    with ExitStack() as ctx:
        keep = ctx.enter_context(tc.tile_pool(name="keep", bufs=1))
        stage = ctx.enter_context(tc.tile_pool(name="stage", bufs=3))
        mx_pool = ctx.enter_context(tc.tile_pool(name="mx_pool", bufs=2))
        psum = ctx.enter_context(tc.psum_pool(name="psum", bufs=PSUM_BANKS))
        ctx.enter_context(tc.manual_schedule())

        bias_rows = keep.tile([P, P], BF16)
        nc.gpsimd.memset(bias_rows[:], 0.0)
        ident_f32 = keep.tile([P, P], F32)
        make_identity(nc, ident_f32[:])
        ident_bf16 = keep.tile([P, P], BF16)
        nc.vector.tensor_copy(out=ident_bf16[:], in_=ident_f32[:])

        x_sb = keep.tile([P, N_TILES * D_IN], BF16)
        h_sb = keep.tile([P, N_TILES * HID], BF16)
        s_sb = keep.tile([P, N_TILES * HID], BF16)
        c_sb = keep.tile([P, N_TILES, HID], BF16)
        w_in_sb = keep.tile([P, N_GATES * 2 * D_IN], BF16)
        w_rec_sb = keep.tile([P, N_GATES * 2 * HID], BF16)
        mask_sb = keep.tile([P, N_TILES], BF16)

        def load_batch(tile_sb, dram, first, count):
            view = tile_sb[:].rearrange("p (t n) -> p t n", t=N_TILES)
            nc.sync.dma_start(
                out=view[:, first : first + count, :],
                in_=by_batch_tile(dram)[:, first : first + count, :],
            )

        def load_gate(tile_sb, rows, gate):
            width = rows.shape[1]
            nc.sync.dma_start(
                out=tile_sb[:, gate * 2 * width : (gate + 1) * 2 * width].rearrange(
                    "p (r n) -> p r n", r=2
                ),
                in_=rows.rearrange("(r p) n -> p r n", p=P),
            )

        def load_in_weights(gate):
            load_gate(w_in_sb, weight_ih[gate * HID : (gate + 1) * HID, :], gate)

        def load_recurrent_weights(gate):
            if gate < N_RECURRENT:
                load_gate(w_rec_sb, weight_hh[gate * HID : (gate + 1) * HID, :], gate)
            else:
                share = gate - N_RECURRENT
                load_gate(w_rec_sb, weight_sh[share * HID : (share + 1) * HID, :], gate)

        def as_rows(vector):
            return vector.rearrange("(r n) -> r n", n=P)

        rec_rows = N_RECURRENT * HID // P
        warm = keep.tile([P, 1], F32)
        nc.vector.memset(warm[:], 0.0)
        nc.scalar.activation(out=warm[:], in_=warm[:], func=ACT.Sigmoid)
        load_in_weights(0)
        load_batch(x_sb, x, 0, 2)
        load_batch(x_sb, x, 2, 2)
        load_in_weights(1)
        nc.sync.dma_start(out=bias_rows[0:GATE_TILES, :], in_=as_rows(bias_ih))
        nc.sync.dma_start(out=bias_rows[GATE_TILES : GATE_TILES + rec_rows, :], in_=as_rows(bias_hh))
        nc.sync.dma_start(out=bias_rows[GATE_TILES + rec_rows : 2 * GATE_TILES, :], in_=as_rows(bias_sh))
        load_recurrent_weights(0)
        load_recurrent_weights(1)
        load_batch(h_sb, h_minors, 0, SIDE)
        load_batch(x_sb, x, SIDE, SIDE)
        load_in_weights(2)
        load_in_weights(3)
        load_batch(h_sb, h_minors, SIDE, SIDE)
        load_recurrent_weights(2)
        load_recurrent_weights(3)
        nc.sync.dma_start(out=mask_sb[:], in_=mask.rearrange("(p t) -> p t", t=N_TILES))
        nc.sync.dma_start(out=c_sb[:], in_=by_batch_tile(c_minors))
        load_in_weights(4)
        load_in_weights(5)
        load_recurrent_weights(4)
        load_recurrent_weights(5)
        load_batch(s_sb, s_minors[idx, :, :], 0, N_TILES)

        bias_col = keep.tile([P, GATE_TILES], F32)

        def turn_biases():
            bias_turned = psum.tile([P, P], BF16, tag="bank")
            nc.tensor.transpose(bias_turned[:], bias_rows[:], ident_bf16[:])
            bias_parts = keep.tile([P, 2 * GATE_TILES], F32)
            nc.vector.tensor_copy(out=bias_parts[:], in_=bias_turned[:, 0 : 2 * GATE_TILES])
            nc.vector.tensor_tensor(
                out=bias_col[:], in0=bias_parts[:, 0:GATE_TILES], in1=bias_parts[:, GATE_TILES:], op=ALU.add
            )

        mask_f32 = keep.tile([P, N_TILES], F32)
        nc.gpsimd.tensor_copy(out=mask_f32[:], in_=mask_sb[:])

        x_codes = keep.tile([P, N_TILES * P], U32, align_bytes=64)
        x_scales = keep.tile([P, N_TILES * P], U8, align_bytes=64)
        w_codes = keep.tile([P, N_GATES * HID], U32, align_bytes=64)
        w_scales = keep.tile([P, N_GATES * HID], U8, align_bytes=64)
        h_T_words = keep.tile([P, N_TILES * P], F32)
        s_T_words = keep.tile([P, N_TILES * P], F32)
        w_rec_T_words = keep.tile([P, N_PAIRS * PAIR_COLS], F32)
        h_T = h_T_words[:].bitcast(BF16).rearrange("p (t b e) -> p t b e", t=N_TILES, e=2)
        s_T = s_T_words[:].bitcast(BF16).rearrange("p (t b e) -> p t b e", t=N_TILES, e=2)
        w_rec_T = w_rec_T_words[:].bitcast(BF16).rearrange("p (g n e) -> p g n e", g=N_PAIRS, e=2)

        def turn_two_blocks(source_sb, first_block, copy_out):
            words = source_sb[:].bitcast(F32)
            turned = psum.tile([P, 2, 2, P], F32, tag="bank")
            for j in range(2):
                for u in range(2):
                    first = (first_block + j) * WORDS + u * P
                    nc.tensor.transpose(turned[:, j, u, :], words[:, first : first + P], ident_f32[:])
            grouped = stage.tile([P, 2 * P * PACK], BF16, align_bytes=64)
            copy_out(
                out=grouped[:].bitcast(F32).rearrange("p (j r u) -> p j r u", j=2, u=2),
                in_=turned[:].rearrange("p j u r -> p j r u"),
            )
            return grouped

        def quantise_two_blocks(grouped, codes, scales, first_block):
            cols = slice(first_block * P, (first_block + 2) * P)
            nc.vector.quantize_mx(
                out=codes[:, cols].bitcast(FP8X4), scales=scales[:, cols], in_=grouped[:]
            )

        def turn_four_blocks(source_sb, dest_words, first_block, copy_out):
            words = source_sb[:].bitcast(F32)
            turned = psum.tile([P, SIDE * P], F32, tag="bank")
            for i in range(SIDE):
                cols = slice((first_block + i) * P, (first_block + i + 1) * P)
                nc.tensor.transpose(turned[:, i * P : (i + 1) * P], words[:, cols], ident_f32[:])
            copy_out(out=dest_words[:, first_block * P : (first_block + SIDE) * P], in_=turned[:])

        def mx_products(pair, half):
            mx_T = mx_pool.tile([P, SIDE, HALF_COLS], F32)
            batch = slice(half * HALF_COLS, (half + 1) * HALF_COLS)
            banks = []
            for j in range(SIDE):
                gate_tile = SIDE * pair + j
                rows = slice(gate_tile * P, (gate_tile + 1) * P)
                acc_mx = psum.tile([P, HALF_COLS], F32, tag="bank")
                nc.tensor.matmul_mx(
                    out=acc_mx[:],
                    lhsT=w_codes[:, rows].bitcast(FP8X4),
                    lhsT_scale=w_scales[:, rows],
                    rhs=x_codes[:, batch].bitcast(FP8X4),
                    rhs_scale=x_scales[:, batch],
                    start=True,
                    stop=True,
                )
                banks.append(acc_mx)
            for j in range(SIDE):
                bias = bias_col[:, SIDE * pair + j : SIDE * pair + j + 1]
                if j % 2 == 0:
                    nc.scalar.activation(out=mx_T[:, j, :], in_=banks[j][:], func=ACT.Identity, bias=bias)
                else:
                    nc.vector.tensor_scalar_add(out=mx_T[:, j, :], in0=banks[j][:], scalar1=bias)
            return mx_T

        steps = [
            (pair, half * SIDE + q)
            for pair in range(N_PAIRS)
            for half in range(N_HALVES)
            for q in range(SIDE)
        ]
        gates = keep.tile([P, N_PAIRS, N_TILES, PAIR_COLS], F32)
        mx_T_of = {}
        pre_of = {}

        def plain_pass(pair, t, c):
            if c == 0:
                bank = psum.tile([P, PAIR_COLS], F32, tag="bank")
                pre_of[(pair, t)] = bank
            state_T = h_T if 2 * pair < N_RECURRENT else s_T
            nc.tensor.matmul(
                out=pre_of[(pair, t)][:],
                lhsT=state_T[:, t, :, c],
                rhs=w_rec_T[:, pair, :, c],
                start=(c == 0),
                stop=False,
            )

        def add_mx_product(pair, t, j):
            q = t % SIDE
            nc.tensor.matmul(
                out=pre_of[(pair, t)][:, j * P : (j + 1) * P],
                lhsT=mx_T_of[(pair, t // SIDE)][:, j, q * P : (q + 1) * P],
                rhs=ident_f32[:],
                is_transpose=True,
                start=False,
                stop=(j == SIDE - 1),
            )

        def activations(pair, t):
            pre = pre_of[(pair, t)]
            if pair == 1:
                nc.scalar.activation(out=gates[:, pair, t, 0:HID], in_=pre[:, 0:HID], func=ACT.Sigmoid)
                nc.scalar.activation(out=gates[:, pair, t, HID:], in_=pre[:, HID:], func=ACT.Tanh)
            else:
                nc.scalar.activation(out=gates[:, pair, t, :], in_=pre[:], func=ACT.Sigmoid)

        kept = keep.tile([P, N_TILES, HID], F32)
        cell = keep.tile([P, N_TILES, HID], F32)
        squashed = keep.tile([P, N_TILES, HID], F32)
        h_res = keep.tile([P, N_TILES, HID], F32)
        c_res = keep.tile([P, N_TILES, HID], F32)
        s_res = keep.tile([P, 2, N_TILES, HID], F32)

        def store(dram, result, t):
            nc.sync.dma_start(out=by_batch_tile(dram)[:, t, :], in_=result[:, t, :])

        def times_masked_tanh(out, gate, t):
            nc.vector.scalar_tensor_tensor(
                out=out,
                in0=squashed[:, t, :],
                scalar=mask_f32[:, t : t + 1],
                in1=gate,
                op0=ALU.mult,
                op1=ALU.mult,
            )

        def products(pair, t):
            if pair == 0:
                nc.vector.tensor_tensor(
                    out=kept[:, t, :], in0=gates[:, 0, t, HID:], in1=c_sb[:, t, :], op=ALU.mult
                )
            elif pair == 1:
                in_term = stage.tile([P, HID], F32)
                nc.vector.tensor_tensor(
                    out=in_term[:], in0=gates[:, 0, t, 0:HID], in1=gates[:, 1, t, HID:], op=ALU.mult
                )
                nc.vector.tensor_tensor(out=cell[:, t, :], in0=in_term[:], in1=kept[:, t, :], op=ALU.add)
            else:
                for share in range(2):
                    times_masked_tanh(s_res[:, share, t, :], gates[:, 2, t, share * HID : (share + 1) * HID], t)
                store(out_s0, s_res[:, 0, :, :], t)
                store(out_s1, s_res[:, 1, :, :], t)

        def new_cell(pair, t):
            if pair == 1:
                m = mask_f32[:, t : t + 1]
                nc.scalar.activation(out=squashed[:, t, :], in_=cell[:, t, :], func=ACT.Tanh, scale=m)
                nc.vector.tensor_scalar_mul(out=c_res[:, t, :], in0=cell[:, t, :], scalar1=m)
                store(out_c, c_res, t)

        def new_hidden(pair, t):
            if pair == 1:
                times_masked_tanh(h_res[:, t, :], gates[:, 1, t, 0:HID], t)
                store(out_h, h_res, t)

        first_w = turn_two_blocks(w_in_sb, 0, nc.vector.tensor_copy)
        first_x = turn_two_blocks(x_sb, 0, nc.scalar.copy)
        second_x = turn_two_blocks(x_sb, 2, nc.vector.tensor_copy)
        quantise_two_blocks(first_w, w_codes, w_scales, 0)
        second_w = turn_two_blocks(w_in_sb, 2, nc.scalar.copy)
        quantise_two_blocks(first_x, x_codes, x_scales, 0)
        quantise_two_blocks(second_x, x_codes, x_scales, 2)
        turn_four_blocks(w_rec_sb, w_rec_T_words, 0, nc.scalar.copy)
        turn_four_blocks(h_sb, h_T_words, 0, nc.vector.tensor_copy)
        turn_biases()
        quantise_two_blocks(second_w, w_codes, w_scales, 2)
        mx_T_of[(0, 0)] = mx_products(0, 0)
        third_x = turn_two_blocks(x_sb, 4, nc.vector.tensor_copy)
        fourth_x = turn_two_blocks(x_sb, 6, nc.scalar.copy)
        quantise_two_blocks(third_x, x_codes, x_scales, 4)
        quantise_two_blocks(fourth_x, x_codes, x_scales, 6)

        waiting = []

        def prepare_in_weights(gate):
            grouped = turn_two_blocks(w_in_sb, 2 * gate, nc.vector.tensor_copy)
            waiting.append(lambda: quantise_two_blocks(grouped, w_codes, w_scales, 2 * gate))

        jobs = [lambda gate=gate: prepare_in_weights(gate) for gate in (2, 3)]
        jobs.append(lambda: turn_four_blocks(h_sb, h_T_words, SIDE, nc.vector.tensor_copy))
        jobs.append(lambda: turn_four_blocks(w_rec_sb, w_rec_T_words, SIDE, nc.vector.tensor_copy))
        jobs += [lambda gate=gate: prepare_in_weights(gate) for gate in (4, 5)]
        jobs.append(lambda: turn_four_blocks(w_rec_sb, w_rec_T_words, 2 * SIDE, nc.vector.tensor_copy))
        jobs.append(lambda: turn_four_blocks(s_sb, s_T_words, 0, nc.vector.tensor_copy))
        jobs.append(lambda: turn_four_blocks(s_sb, s_T_words, SIDE, nc.vector.tensor_copy))

        def lagged(stage_of_step, n, lag):
            if 0 <= n - lag < len(steps):
                stage_of_step(*steps[n - lag])

        for c in range(K_CHUNKS):
            plain_pass(*steps[0], c)
        for n in range(len(steps) + 4):
            if n < len(steps):
                pair, t = steps[n]
                block = n // SIDE
                if n % SIDE == MX_AT and block + 1 < N_PAIRS * N_HALVES:
                    ahead = divmod(block + 1, N_HALVES)
                    mx_T_of[ahead] = mx_products(*ahead)
                for c in range(K_CHUNKS):
                    if n + 1 < len(steps):
                        plain_pass(*steps[n + 1], c)
                    add_mx_product(pair, t, 2 * c)
                    add_mx_product(pair, t, 2 * c + 1)
                while waiting:
                    waiting.pop(0)()
                if n < len(jobs):
                    jobs[n]()
            lagged(activations, n, 1)
            lagged(products, n, 2)
            lagged(new_cell, n, 3)
            lagged(new_hidden, n, 4)
